import numpy as np
import ml_dtypes


def mxq(x, axis, fmt="e4m3"):
    dtype, down = {"e4m3": (ml_dtypes.float8_e4m3fn, 7), "e5m2": (ml_dtypes.float8_e5m2, 14)}[fmt]
    v = np.moveaxis(np.asarray(x, np.float32).astype(ml_dtypes.bfloat16).astype(np.float64), axis, -1)
    blocks = v.reshape(v.shape[:-1] + (-1, 32))
    amax = np.abs(blocks).max(-1, keepdims=True)
    byte = np.maximum(np.where(amax > 0, np.frexp(amax)[1] - 1 + 127, 0) - down, 1)
    scale = np.exp2(byte - 127.0)
    codes = (blocks / scale).astype(np.float32).astype(dtype).astype(np.float64)
    return np.moveaxis((codes * scale).reshape(v.shape), -1, axis)


WIDE = False


def mx_kscale(k):
    if not WIDE:
        return np.ones(k)
    levels = np.array([18, -18])
    if k % 512:
        return np.exp2(np.random.permutation(np.resize(levels, k // 32))).repeat(32)
    a = np.empty((k // 512, 16))
    for p in range(k // 512):
        a[p, :8] = np.random.permutation(np.resize(levels, 8))
        for g in range(8):
            far = levels[np.abs(levels - a[p, g]) >= 10]
            a[p, g + 8] = far[np.random.randint(len(far))]
    return np.exp2(a.ravel()).repeat(32)


BF16 = ml_dtypes.bfloat16


def bf(x):
    return np.asarray(x, np.float32).astype(BF16)


def f64(x):
    return np.asarray(x).astype(np.float64)


B, N, IN_DIM = 8, 512, 512
EPS = 1e-6
SIG = 2.0


def inv_sqrt_degree(adj):
    return (adj.sum(axis=2) + EPS) ** -0.5


def laplacian(adj, r):
    return np.eye(N)[None] - r[:, :, None] * adj * r[:, None, :]


def setup_inputs():
    s = mx_kscale(N)
    u = mx_kscale(IN_DIM)
    x0 = bf(np.random.standard_normal((B, N, IN_DIM)))
    adj0 = bf(np.exp(SIG * np.random.standard_normal((B, N, N)) - SIG * SIG / 2.0) / N)
    g = bf(np.random.standard_normal((B, N, IN_DIM)) * np.exp2(np.random.randint(-6, 1, (B, N, 1))) / s[:, None] * u * np.min(s))
    r = inv_sqrt_degree(f64(adj0))
    return {"x": bf(f64(x0) / u),
            "adj": bf(f64(adj0) * s[:, None] / s[None, :]),
            "r": np.asarray(r, np.float32),
            "grad_out": g}


def reference(x, adj, r, grad_out):
    a = f64(adj)
    rf = f64(r)
    g = f64(grad_out)
    L = laplacian(a, rf)
    dx = np.swapaxes(mxq(L, 1, "e4m3"), 1, 2) @ mxq(g, 1, "e5m2")
    dL = mxq(g, 2, "e5m2") @ np.swapaxes(mxq(f64(x), 2, "e4m3"), 1, 2)
    p = dL * a
    dr = -(p * rf[:, None, :]).sum(axis=2) - (p * rf[:, :, None]).sum(axis=1)
    dd = -0.5 * rf ** 3 * dr
    dadj = dd[:, :, None] - rf[:, :, None] * dL * rf[:, None, :]
    return dx, dadj

@@ -1,0 +1,371 @@
+from contextlib import ExitStack
+
+import concourse.mybir as mybir
+from concourse.masks import make_identity
+
+B, N, D = 8, 512, 512
+FLOPS = 2 * 2 * B * N * N * D
+
+F32 = mybir.dt.float32
+BF16 = mybir.dt.bfloat16
+U32 = mybir.dt.uint32
+U8 = mybir.dt.uint8
+E4M3 = mybir.dt.float8_e4m3fn_x4
+E5M2 = mybir.dt.float8_e5m2_x4
+ALU = mybir.AluOpType
+
+P = 128
+PACK = 4
+AHEAD = 3
+S_COLS = 256
+SUM_N = 64
+
+
+def tile_cheblayer_pa_v_kernel(tc, x, adj, r, grad_out, out_0, out_1):
+    nc = tc.nc
+
+    with ExitStack() as ctx:
+        const = ctx.enter_context(tc.tile_pool(name="const", bufs=1))
+        inp = ctx.enter_context(tc.tile_pool(name="inp", bufs=AHEAD + 2))
+        work = ctx.enter_context(tc.tile_pool(name="work", bufs=3))
+        stage = ctx.enter_context(tc.tile_pool(name="stage", bufs=2))
+        prod = ctx.enter_context(tc.tile_pool(name="prod", bufs=4))
+        ps_move = ctx.enter_context(tc.psum_pool(name="ps_move", bufs=4))
+        ps_dl = ctx.enter_context(tc.psum_pool(name="ps_dl", bufs=2))
+        ps_one = ctx.enter_context(tc.psum_pool(name="ps_one", bufs=1))
+        ctx.enter_context(tc.manual_schedule())
+
+        a_sb, g_sb, x_sb, banks, staged, quant = {}, {}, {}, {}, {}, {}
+        r_ps, r_row, neg_m, dl_ps, dl_r, q, row_sum, sum_ps, dd, dx = {}, {}, {}, {}, {}, {}, {}, {}, {}, {}
+
+        def rows(hbm, g):
+            return hbm[g].rearrange("(p t) w -> p t w", t=PACK)
+
+        def load_rows(hbm, g, name, parts):
+            flat = inp.tile([P, PACK * D], BF16, name=name, align_bytes=64)
+            view = flat[:].rearrange("p (t w) -> p t w", t=PACK)
+            step = PACK // parts
+            for t in range(0, PACK, step):
+                nc.sync.dma_start(out=view[:, t : t + step, :], in_=rows(hbm, g)[:, t : t + step, :])
+            return view
+
+        def load(g):
+            x_sb[g] = load_rows(x, g, "x_sb", 1)
+            g_sb[g] = load_rows(grad_out, g, "g_sb", 1)
+            a_sb[g] = load_rows(adj, g, "a_sb", 1)
+
+        r_first = const.tile([P, 1, PACK], F32, name="r_first")
+        r_rest = const.tile([P, B - 1, PACK], F32, name="r_rest")
+        r_hbm = r.rearrange("g (p t) -> p g t", t=PACK)
+        nc.sync.dma_start(out=r_first[:], in_=r_hbm[:, 0:1, :])
+        x_sb[0] = load_rows(x, 0, "x_sb", 2)
+        a_sb[0] = load_rows(adj, 0, "a_sb", 2)
+        g_sb[0] = load_rows(grad_out, 0, "g_sb", 2)
+        nc.sync.dma_start(out=r_rest[:], in_=r_hbm[:, 1:B, :])
+        for g in range(1, AHEAD):
+            load(g)
+
+        ident = const.tile([P, P], F32, name="ident")
+        make_identity(nc, ident[:])
+        ones = const.tile([P, SUM_N], F32, name="ones")
+        nc.vector.memset(ones[:], 1.0)
+        neg_r = const.tile([P, B, PACK], F32, name="neg_r")
+        dd_gain = const.tile([P, B, PACK], F32, name="dd_gain")
+
+        def degree_constants(r_col, graphs):
+            nc.vector.tensor_scalar(
+                out=neg_r[:, graphs, :], in0=r_col[:], scalar1=-1.0, scalar2=None, op0=ALU.mult
+            )
+            nc.vector.scalar_tensor_tensor(
+                out=dd_gain[:, graphs, :],
+                in0=r_col[:],
+                scalar=-0.5,
+                in1=r_col[:],
+                op0=ALU.mult,
+                op1=ALU.mult,
+            )
+
+        def transpose_words(key, src, h):
+            bank = ps_move.tile([P, 2, 2, P], F32, name="move")
+            for tt in range(2):
+                words = src[:, 2 * h + tt, :].bitcast(F32)
+                for u in range(2):
+                    nc.tensor.transpose(bank[:, tt, u, :], words[:, u : D // 2 : 2], ident[:])
+            banks[key, h] = bank
+
+        def copy_words_out(key, h):
+            if h == 0:
+                staged[key] = stage.tile([P, PACK * N], BF16, name="st_" + key[0], align_bytes=64)
+            words = staged[key][:].bitcast(F32).rearrange("p (h t c u) -> p h t c u", h=2, t=2, u=2)
+            nc.scalar.copy(out=words[:, h], in_=banks[key, h][:].rearrange("p t u c -> p t c u"))
+
+        def quantize(key, fmt, src, first):
+            if first == 0:
+                codes = stage.tile([P, N], U32, name="codes_" + key[0], align_bytes=64)
+                scales = stage.tile([P, N], U8, name="scales_" + key[0], align_bytes=64)
+                quant[key] = (codes, scales, fmt)
+            codes, scales, fmt = quant[key]
+            cols = slice(first, first + src.shape[1] // PACK)
+            nc.vector.quantize_mx(out=codes[:, cols].bitcast(fmt), scales=scales[:, cols], in_=src)
+
+        def mx_pass(acc, lhs_key, t, rhs_key):
+            lc, ls, lf = quant[lhs_key]
+            rc, rs, rf = quant[rhs_key]
+            cols = slice(t * P, (t + 1) * P)
+            nc.tensor.matmul_mx(
+                out=acc[:],
+                lhsT=lc[:, cols].bitcast(lf),
+                lhsT_scale=ls[:, cols],
+                rhs=rc[:].bitcast(rf),
+                rhs_scale=rs[:],
+                start=True,
+                stop=True,
+            )
+
+        def dl_matmul(g, t):
+            dl_ps[g, t] = ps_dl.tile([P, N], F32, name="dl")
+            mx_pass(dl_ps[g, t], ("gT", g), t, ("xT", g))
+
+        def spread_r(g):
+            r_ps[g] = ps_one.tile([P, PACK, P], F32, name="r_ps")
+            r_col = r_first[:, 0, :] if g == 0 else r_rest[:, g - 1, :]
+            for t in range(PACK):
+                nc.tensor.transpose(r_ps[g][:, t, :], r_col[:, t : t + 1].to_broadcast([P, P]), ident[:])
+
+        def copy_r_row(g):
+            r_row[g] = stage.tile([P, P, PACK], F32, name="r_row")
+            nc.scalar.copy(out=r_row[g][:], in_=r_ps[g][:].rearrange("p t c -> p c t"))
+
+        def scale_adj(g, t):
+            if t == 0:
+                neg_m[g] = work.tile([P, PACK, PACK, P], F32, name="neg_m")
+            nc.vector.scalar_tensor_tensor(
+                out=neg_m[g][:, t],
+                in0=a_sb[g][:, t, :].rearrange("p (c t) -> p t c", t=PACK),
+                scalar=neg_r[:, g, t : t + 1],
+                in1=r_ps[g][:],
+                op0=ALU.mult,
+                op1=ALU.mult,
+            )
+
+        def interleave_scalar(g):
+            nc.scalar.copy(
+                out=staged["gI", g][:, 0 : PACK * S_COLS].rearrange("p (c i t) -> p c t i", i=4, t=PACK),
+                in_=g_sb[g][:, :, 0:S_COLS].rearrange("p t (c i) -> p c t i", i=4),
+            )
+
+        def interleave_gpsimd(g):
+            staged["gI", g] = stage.tile([P, PACK * D], BF16, name="st_gI", bufs=1, align_bytes=64)
+            nc.gpsimd.tensor_scalar(
+                out=staged["gI", g][:, PACK * S_COLS : PACK * D].rearrange("p (w t) -> p w t", t=PACK),
+                in0=g_sb[g][:, :, S_COLS:D].rearrange("p t w -> p w t"),
+                scalar1=1.0,
+                scalar2=0.0,
+                op0=ALU.mult,
+                op1=ALU.add,
+            )
+
+        def add_identity(engine, g, t0, t1, eye):
+            diag = neg_m[g][:].rearrange("p t s c -> p (t s) c")[:, t0 * (PACK + 1) : (t1 - 1) * (PACK + 1) + 1 : PACK + 1, :]
+            engine.tensor_tensor(
+                out=diag, in0=diag, in1=eye[:].unsqueeze(1).to_broadcast([P, t1 - t0, P]), op=ALU.add
+            )
+
+        def round_laplacian(g, s0, s1):
+            if s0 == 0:
+                staged["L", g] = stage.tile([P, PACK * N], BF16, name="st_L", align_bytes=64)
+            nc.scalar.copy(
+                out=staged["L", g][:, s0 * N : s1 * N].rearrange("p (c i t) -> p c t i", i=4, t=PACK),
+                in_=neg_m[g][:]
+                .rearrange("p t s c -> p t (s c)")[:, :, s0 * P : s1 * P]
+                .rearrange("p t (c i) -> p c t i", i=4),
+            )
+
+        def weigh_dl(g, t):
+            if t == 0:
+                row_sum[g] = stage.tile([P, PACK], F32, name="row_sum")
+            q[g, t] = prod.tile([P, N], F32, name="q")
+            nc.vector.scalar_tensor_tensor(
+                out=q[g, t][:],
+                in0=dl_ps[g, t][:],
+                scalar=1.0,
+                in1=neg_m[g][:, t].rearrange("p s c -> p (s c)"),
+                op0=ALU.mult,
+                op1=ALU.mult,
+                accum_out=row_sum[g][:, t : t + 1],
+            )
+
+        def scale_dl(g, t):
+            if t == 0:
+                dl_r[g] = work.tile([P, PACK, N], F32, name="dl_r")
+            nc.vector.tensor_tensor(
+                out=dl_r[g][:, t, :].rearrange("p (c s) -> p c s", s=PACK),
+                in0=dl_ps[g, t][:].rearrange("p (s c) -> p c s", s=PACK),
+                in1=r_row[g][:],
+                op=ALU.mult,
+            )
+
+        def column_sums(g, t):
+            if t == 0:
+                sum_ps[g] = ps_one.tile([P, PACK, SUM_N], F32, name="sum_ps")
+            for s in range(PACK):
+                nc.tensor.matmul(
+                    sum_ps[g][:, s, :],
+                    lhsT=q[g, t][:, s * P : (s + 1) * P],
+                    rhs=ones[:],
+                    start=(t == 0 and s == 0),
+                    stop=False,
+                )
+            if t == PACK - 1:
+                nc.tensor.matmul(sum_ps[g][:, :, 0], lhsT=ident[:], rhs=row_sum[g][:], start=False, stop=True)
+
+        def degree_term(g):
+            dd[g] = stage.tile([P, PACK], F32, name="dd")
+            nc.vector.tensor_tensor(out=dd[g][:], in0=sum_ps[g][:, :, 0], in1=dd_gain[:, g, :], op=ALU.mult)
+
+        def finish_adj(engine, g, t):
+            engine.tensor_scalar(
+                out=dl_r[g][:, t, :],
+                in0=dl_r[g][:, t, :],
+                scalar1=neg_r[:, g, t : t + 1],
+                scalar2=dd[g][:, t : t + 1],
+                op0=ALU.mult,
+                op1=ALU.add,
+            )
+
+        def store_adj(g, t0, t1):
+            nc.sync.dma_start(out=rows(out_1, g)[:, t0:t1, :], in_=dl_r[g][:, t0:t1, :])
+
+        def dx_matmul(g, s):
+            banks["dx", g, s] = ps_move.tile([P, D], F32, name="move")
+            mx_pass(banks["dx", g, s], ("L", g), s, ("gI", g))
+
+        def copy_dx_out(g, s):
+            if s == 0:
+                dx[g] = work.tile([P, PACK, D], F32, name="dx")
+            nc.scalar.copy(out=dx[g][:, s, :], in_=banks["dx", g, s][:])
+
+        def store_dx(g, s0, s1):
+            nc.sync.dma_start(out=rows(out_0, g)[:, s0:s1, :], in_=dx[g][:, s0:s1, :])
+
+        def moves(g):
+            return [((name, g), src[g], h) for name, src in (("xT", x_sb), ("gT", g_sb)) for h in range(2)]
+
+        degree_constants(r_first, slice(0, 1))
+        spread_r(0)
+        for key, src, h in moves(0):
+            transpose_words(key, src, h)
+            copy_words_out(key, h)
+
+        last = B - 1
+        half = PACK // 2
+        for g in range(B):
+            prev, nxt = g - 1, g + 1
+            ahead = moves(nxt) if g < last else []
+            if g + AHEAD < B:
+                load(g + AHEAD)
+            if g > 0:
+                for key, src, h in ahead:
+                    transpose_words(key, src, h)
+                add_identity(nc.gpsimd, prev, half, PACK, ident)
+                round_laplacian(prev, half, PACK)
+            scale_adj(g, 0)
+            scale_adj(g, 1)
+            if g > 0:
+                degree_term(prev)
+                finish_adj(nc.gpsimd, prev, 0)
+            scale_adj(g, 2)
+            scale_adj(g, 3)
+            quantize(("xT", g), E4M3, staged["xT", g][:], 0)
+            if g == 0:
+                copy_r_row(g)
+                quantize(("gT", g), E5M2, staged["gT", g][:, 0 : half * N], 0)
+                dl_matmul(g, 0)
+                dl_matmul(g, 1)
+                quantize(("gT", g), E5M2, staged["gT", g][:, half * N : PACK * N], half * P)
+                degree_constants(r_rest, slice(1, B))
+            else:
+                quantize(("gT", g), E5M2, staged["gT", g][:], 0)
+                if g < last:
+                    spread_r(nxt)
+                dl_matmul(g, 0)
+                dl_matmul(g, 1)
+                for key, src, h in ahead:
+                    copy_words_out(key, h)
+                if g < last:
+                    copy_r_row(nxt)
+                quantize(("L", prev), E4M3, staged["L", prev][:], 0)
+                quantize(("gI", prev), E5M2, staged["gI", prev][:], 0)
+                for s in range(PACK):
+                    dx_matmul(prev, s)
+                for s in range(PACK):
+                    copy_dx_out(prev, s)
+                    if s % 2 == 1:
+                        store_dx(prev, s - 1, s + 1)
+            if g > 0:
+                interleave_gpsimd(g)
+                interleave_scalar(g)
+            if g < last:
+                for t in range(PACK):
+                    if g == 0:
+                        transpose_words(*ahead[t])
+                        copy_words_out(ahead[t][0], ahead[t][2])
+                        if t == 1:
+                            spread_r(nxt)
+                            copy_r_row(nxt)
+                    weigh_dl(g, t)
+                    scale_dl(g, t)
+                    if t + 2 < PACK:
+                        dl_matmul(g, t + 2)
+                    column_sums(g, t)
+                    if t == half:
+                        add_identity(nc.gpsimd, g, 0, half, ident)
+                        round_laplacian(g, 0, half)
+                        if g == 0:
+                            interleave_gpsimd(g)
+                            interleave_scalar(g)
+                    if g > 0 and t + 1 < PACK:
+                        finish_adj(nc.gpsimd, prev, t + 1)
+                        if t % 2 == 0:
+                            store_adj(prev, t, t + 2)
+
+        g = last
+        for t in range(1, PACK):
+            finish_adj(nc.gpsimd, g - 1, t)
+            if t % 2 == 1:
+                store_adj(g - 1, t - 1, t + 1)
+        ident_ps = ps_one.tile([P, P], F32, name="r_ps")
+        nc.tensor.transpose(ident_ps[:], ident[:], ident[:])
+        for t in range(half):
+            weigh_dl(g, t)
+            scale_dl(g, t)
+            add_identity(nc.vector, g, t, t + 1, ident_ps)
+            dl_matmul(g, t + 2)
+            column_sums(g, t)
+            round_laplacian(g, t, t + 1)
+        for t in range(half, PACK):
+            weigh_dl(g, t)
+            column_sums(g, t)
+        add_identity(nc.vector, g, half, PACK, ident_ps)
+        round_laplacian(g, half, PACK)
+        quantize(("gI", g), E5M2, staged["gI", g][:], 0)
+        quantize(("L", g), E4M3, staged["L", g][:, 0 : half * N], 0)
+        for t in range(half):
+            dx_matmul(g, t)
+            copy_dx_out(g, t)
+            store_dx(g, t, t + 1)
+        scale_dl(g, 2)
+        degree_term(g)
+        quantize(("L", g), E4M3, staged["L", g][:, half * N : PACK * N], half * P)
+        for t in range(half, PACK):
+            dx_matmul(g, t)
+        finish_adj(nc.vector, g, 0)
+        store_adj(g, 0, 1)
+        finish_adj(nc.vector, g, 1)
+        store_adj(g, 1, 2)
+        scale_dl(g, 3)
+        for t in range(half, PACK):
+            copy_dx_out(g, t)
+            store_dx(g, t, t + 1)
+            finish_adj(nc.vector, g, t)
+            store_adj(g, t, t + 1)

@@ -13,12 +13,15 @@ U8 = mybir.dt.uint8
 E4M3 = mybir.dt.float8_e4m3fn_x4
 E5M2 = mybir.dt.float8_e5m2_x4
 ALU = mybir.AluOpType
+ACT = mybir.ActivationFunctionType
 
 P = 128
 PACK = 4
+HALF = PACK // 2
 AHEAD = 3
 S_COLS = 256
 SUM_N = 64
+DL_BANK, R_BANK, SUM_BANK = 4, 6, 7
 
 
 def tile_cheblayer_pa_v_kernel(tc, x, adj, r, grad_out, out_0, out_1):
@@ -30,37 +33,41 @@ def tile_cheblayer_pa_v_kernel(tc, x, adj, r, grad_out, out_0, out_1):
         work = ctx.enter_context(tc.tile_pool(name="work", bufs=3))
         stage = ctx.enter_context(tc.tile_pool(name="stage", bufs=2))
         prod = ctx.enter_context(tc.tile_pool(name="prod", bufs=4))
-        ps_move = ctx.enter_context(tc.psum_pool(name="ps_move", bufs=4))
-        ps_dl = ctx.enter_context(tc.psum_pool(name="ps_dl", bufs=2))
-        ps_one = ctx.enter_context(tc.psum_pool(name="ps_one", bufs=1))
+        psum = ctx.enter_context(tc.psum_pool(name="psum", bufs=1))
         ctx.enter_context(tc.manual_schedule())
 
         a_sb, g_sb, x_sb, banks, staged, quant = {}, {}, {}, {}, {}, {}
         r_ps, r_row, neg_m, dl_ps, dl_r, q, row_sum, sum_ps, dd, dx = {}, {}, {}, {}, {}, {}, {}, {}, {}, {}
 
+        def open_bank(index, shape):
+            return psum.tile(shape, F32, name="bank%d" % index)
+
         def rows(hbm, g):
             return hbm[g].rearrange("(p t) w -> p t w", t=PACK)
 
-        def load_rows(hbm, g, name, parts):
+        def open_rows(name):
             flat = inp.tile([P, PACK * D], BF16, name=name, align_bytes=64)
-            view = flat[:].rearrange("p (t w) -> p t w", t=PACK)
-            step = PACK // parts
-            for t in range(0, PACK, step):
-                nc.sync.dma_start(out=view[:, t : t + step, :], in_=rows(hbm, g)[:, t : t + step, :])
-            return view
+            return flat[:].rearrange("p (t w) -> p t w", t=PACK)
+
+        def load_rows(dst, hbm, g, t0, t1):
+            nc.sync.dma_start(out=dst[:, t0:t1, :], in_=rows(hbm, g)[:, t0:t1, :])
 
         def load(g):
-            x_sb[g] = load_rows(x, g, "x_sb", 1)
-            g_sb[g] = load_rows(grad_out, g, "g_sb", 1)
-            a_sb[g] = load_rows(adj, g, "a_sb", 1)
+            for tiles, hbm, name in ((x_sb, x, "x_sb"), (g_sb, grad_out, "g_sb"), (a_sb, adj, "a_sb")):
+                tiles[g] = open_rows(name)
+                load_rows(tiles[g], hbm, g, 0, PACK)
 
         r_first = const.tile([P, 1, PACK], F32, name="r_first")
         r_rest = const.tile([P, B - 1, PACK], F32, name="r_rest")
         r_hbm = r.rearrange("g (p t) -> p g t", t=PACK)
         nc.sync.dma_start(out=r_first[:], in_=r_hbm[:, 0:1, :])
-        x_sb[0] = load_rows(x, 0, "x_sb", 2)
-        a_sb[0] = load_rows(adj, 0, "a_sb", 2)
-        g_sb[0] = load_rows(grad_out, 0, "g_sb", 2)
+        x_sb[0], g_sb[0], a_sb[0] = open_rows("x_sb"), open_rows("g_sb"), open_rows("a_sb")
+        load_rows(a_sb[0], adj, 0, 0, HALF)
+        load_rows(x_sb[0], x, 0, 0, HALF)
+        load_rows(x_sb[0], x, 0, HALF, PACK)
+        load_rows(g_sb[0], grad_out, 0, 0, HALF)
+        load_rows(a_sb[0], adj, 0, HALF, PACK)
+        load_rows(g_sb[0], grad_out, 0, HALF, PACK)
         nc.sync.dma_start(out=r_rest[:], in_=r_hbm[:, 1:B, :])
         for g in range(1, AHEAD):
             load(g)
@@ -73,9 +80,7 @@ def tile_cheblayer_pa_v_kernel(tc, x, adj, r, grad_out, out_0, out_1):
         dd_gain = const.tile([P, B, PACK], F32, name="dd_gain")
 
         def degree_constants(r_col, graphs):
-            nc.vector.tensor_scalar(
-                out=neg_r[:, graphs, :], in0=r_col[:], scalar1=-1.0, scalar2=None, op0=ALU.mult
-            )
+            nc.scalar.activation(out=neg_r[:, graphs, :], in_=r_col[:], func=ACT.Copy, scale=-1.0)
             nc.vector.scalar_tensor_tensor(
                 out=dd_gain[:, graphs, :],
                 in0=r_col[:],
@@ -85,15 +90,15 @@ def tile_cheblayer_pa_v_kernel(tc, x, adj, r, grad_out, out_0, out_1):
                 op1=ALU.mult,
             )
 
-        def transpose_words(key, src, h):
-            bank = ps_move.tile([P, 2, 2, P], F32, name="move")
+        def transpose_words(key, src, h, index):
+            bank = open_bank(index, [P, 2, 2, P])
             for tt in range(2):
                 words = src[:, 2 * h + tt, :].bitcast(F32)
                 for u in range(2):
                     nc.tensor.transpose(bank[:, tt, u, :], words[:, u : D // 2 : 2], ident[:])
             banks[key, h] = bank
 
-        def copy_words_out(key, h):
+        def copy_words_out(key, src, h, index):
             if h == 0:
                 staged[key] = stage.tile([P, PACK * N], BF16, name="st_" + key[0], align_bytes=64)
             words = staged[key][:].bitcast(F32).rearrange("p (h t c u) -> p h t c u", h=2, t=2, u=2)
@@ -122,12 +127,12 @@ def tile_cheblayer_pa_v_kernel(tc, x, adj, r, grad_out, out_0, out_1):
                 stop=True,
             )
 
-        def dl_matmul(g, t):
-            dl_ps[g, t] = ps_dl.tile([P, N], F32, name="dl")
+        def dl_matmul(g, t, index=None):
+            dl_ps[g, t] = open_bank(DL_BANK + t % 2 if index is None else index, [P, N])
             mx_pass(dl_ps[g, t], ("gT", g), t, ("xT", g))
 
         def spread_r(g):
-            r_ps[g] = ps_one.tile([P, PACK, P], F32, name="r_ps")
+            r_ps[g] = open_bank(R_BANK, [P, PACK, P])
             r_col = r_first[:, 0, :] if g == 0 else r_rest[:, g - 1, :]
             for t in range(PACK):
                 nc.tensor.transpose(r_ps[g][:, t, :], r_col[:, t : t + 1].to_broadcast([P, P]), ident[:])
@@ -148,14 +153,16 @@ def tile_cheblayer_pa_v_kernel(tc, x, adj, r, grad_out, out_0, out_1):
                 op1=ALU.mult,
             )
 
-        def interleave_scalar(g):
+        def open_interleaved(g, name):
+            staged["gI", g] = stage.tile([P, PACK * D], BF16, name=name, bufs=1, align_bytes=64)
+
+        def interleave_scalar(g, cols):
             nc.scalar.copy(
-                out=staged["gI", g][:, 0 : PACK * S_COLS].rearrange("p (c i t) -> p c t i", i=4, t=PACK),
-                in_=g_sb[g][:, :, 0:S_COLS].rearrange("p t (c i) -> p c t i", i=4),
+                out=staged["gI", g][:, 0 : PACK * cols].rearrange("p (c i t) -> p c t i", i=4, t=PACK),
+                in_=g_sb[g][:, :, 0:cols].rearrange("p t (c i) -> p c t i", i=4),
             )
 
         def interleave_gpsimd(g):
-            staged["gI", g] = stage.tile([P, PACK * D], BF16, name="st_gI", bufs=1, align_bytes=64)
             nc.gpsimd.tensor_scalar(
                 out=staged["gI", g][:, PACK * S_COLS : PACK * D].rearrange("p (w t) -> p w t", t=PACK),
                 in0=g_sb[g][:, :, S_COLS:D].rearrange("p t w -> p w t"),
@@ -207,7 +214,7 @@ def tile_cheblayer_pa_v_kernel(tc, x, adj, r, grad_out, out_0, out_1):
 
         def column_sums(g, t):
             if t == 0:
-                sum_ps[g] = ps_one.tile([P, PACK, SUM_N], F32, name="sum_ps")
+                sum_ps[g] = open_bank(SUM_BANK, [P, PACK, SUM_N])
             for s in range(PACK):
                 nc.tensor.matmul(
                     sum_ps[g][:, s, :],
@@ -219,9 +226,26 @@ def tile_cheblayer_pa_v_kernel(tc, x, adj, r, grad_out, out_0, out_1):
             if t == PACK - 1:
                 nc.tensor.matmul(sum_ps[g][:, :, 0], lhsT=ident[:], rhs=row_sum[g][:], start=False, stop=True)
 
-        def degree_term(g):
+        def degree_term(g, t0, t1):
+            if t0 == 0:
+                dd[g] = stage.tile([P, PACK], F32, name="dd")
+            for t in range(t0, t1):
+                nc.scalar.activation(
+                    out=dd[g][:, t : t + 1], in_=sum_ps[g][:, t, 0:1], func=ACT.Copy, scale=dd_gain[:, g, t : t + 1]
+                )
+
+        def degree_term_vector(g):
             dd[g] = stage.tile([P, PACK], F32, name="dd")
             nc.vector.tensor_tensor(out=dd[g][:], in0=sum_ps[g][:, :, 0], in1=dd_gain[:, g, :], op=ALU.mult)
+
+        def finish_adj_scalar(g, t):
+            nc.scalar.activation(
+                out=dl_r[g][:, t, :],
+                in_=dl_r[g][:, t, :],
+                func=ACT.Identity,
+                scale=neg_r[:, g, t : t + 1],
+                bias=dd[g][:, t : t + 1],
+            )
 
         def finish_adj(engine, g, t):
             engine.tensor_scalar(
@@ -236,136 +260,175 @@ def tile_cheblayer_pa_v_kernel(tc, x, adj, r, grad_out, out_0, out_1):
         def store_adj(g, t0, t1):
             nc.sync.dma_start(out=rows(out_1, g)[:, t0:t1, :], in_=dl_r[g][:, t0:t1, :])
 
-        def dx_matmul(g, s):
-            banks["dx", g, s] = ps_move.tile([P, D], F32, name="move")
+        def dx_matmul(g, s, index):
+            banks["dx", g, s] = open_bank(index, [P, D])
             mx_pass(banks["dx", g, s], ("L", g), s, ("gI", g))
 
-        def copy_dx_out(g, s):
+        def copy_dx_out(g, s, copy=nc.scalar.copy):
             if s == 0:
                 dx[g] = work.tile([P, PACK, D], F32, name="dx")
-            nc.scalar.copy(out=dx[g][:, s, :], in_=banks["dx", g, s][:])
+            copy(out=dx[g][:, s, :], in_=banks["dx", g, s][:])
 
         def store_dx(g, s0, s1):
             nc.sync.dma_start(out=rows(out_0, g)[:, s0:s1, :], in_=dx[g][:, s0:s1, :])
 
         def moves(g):
-            return [((name, g), src[g], h) for name, src in (("xT", x_sb), ("gT", g_sb)) for h in range(2)]
+            halves = [((name, g), src[g], h) for name, src in (("xT", x_sb), ("gT", g_sb)) for h in range(2)]
+            return [half + (index,) for index, half in enumerate(halves)]
+
+        last = B - 1
 
         degree_constants(r_first, slice(0, 1))
         spread_r(0)
-        for key, src, h in moves(0):
-            transpose_words(key, src, h)
-            copy_words_out(key, h)
+        for move in moves(0):
+            transpose_words(*move)
+            copy_words_out(*move)
+        for t in range(PACK - 1):
+            scale_adj(0, t)
+        quantize(("xT", 0), E4M3, staged["xT", 0][:], 0)
+        quantize(("gT", 0), E5M2, staged["gT", 0][:, 0 : HALF * N], 0)
+        dl_matmul(0, 0)
+        dl_matmul(0, 1)
+        scale_adj(0, PACK - 1)
+        copy_r_row(0)
+        quantize(("gT", 0), E5M2, staged["gT", 0][:, HALF * N : PACK * N], HALF * P)
+        degree_constants(r_rest, slice(1, B))
+        open_interleaved(0, "st_gI")
+        interleave_scalar(0, S_COLS)
+        ahead = moves(1)
+        for move in ahead[:HALF]:
+            transpose_words(*move)
+            copy_words_out(*move)
+        spread_r(1)
+        copy_r_row(1)
+        for t in range(PACK):
+            weigh_dl(0, t)
+            scale_dl(0, t)
+            if t + 2 < PACK:
+                dl_matmul(0, t + 2)
+            column_sums(0, t)
+            if t < HALF:
+                transpose_words(*ahead[HALF + t])
+                copy_words_out(*ahead[HALF + t])
+            if t == HALF:
+                add_identity(nc.gpsimd, 0, 0, HALF, ident)
+                round_laplacian(0, 0, HALF)
+                interleave_gpsimd(0)
+        load(AHEAD)
 
-        last = B - 1
-        half = PACK // 2
-        for g in range(B):
+        for g in range(1, B):
             prev, nxt = g - 1, g + 1
             ahead = moves(nxt) if g < last else []
             if g + AHEAD < B:
                 load(g + AHEAD)
-            if g > 0:
-                for key, src, h in ahead:
-                    transpose_words(key, src, h)
-                add_identity(nc.gpsimd, prev, half, PACK, ident)
-                round_laplacian(prev, half, PACK)
-            scale_adj(g, 0)
-            scale_adj(g, 1)
-            if g > 0:
-                degree_term(prev)
-                finish_adj(nc.gpsimd, prev, 0)
-            scale_adj(g, 2)
-            scale_adj(g, 3)
+            for move in ahead:
+                transpose_words(*move)
+            add_identity(nc.gpsimd, prev, HALF, PACK, ident)
+            degree_term(prev, 0, PACK if g < last else 1)
+            round_laplacian(prev, HALF, PACK)
+            finish_adj(nc.gpsimd, prev, 0)
+            for t in range(PACK):
+                scale_adj(g, t)
             quantize(("xT", g), E4M3, staged["xT", g][:], 0)
-            if g == 0:
-                copy_r_row(g)
-                quantize(("gT", g), E5M2, staged["gT", g][:, 0 : half * N], 0)
-                dl_matmul(g, 0)
-                dl_matmul(g, 1)
-                quantize(("gT", g), E5M2, staged["gT", g][:, half * N : PACK * N], half * P)
-                degree_constants(r_rest, slice(1, B))
-            else:
-                quantize(("gT", g), E5M2, staged["gT", g][:], 0)
-                if g < last:
-                    spread_r(nxt)
-                dl_matmul(g, 0)
-                dl_matmul(g, 1)
-                for key, src, h in ahead:
-                    copy_words_out(key, h)
-                if g < last:
-                    copy_r_row(nxt)
-                quantize(("L", prev), E4M3, staged["L", prev][:], 0)
-                quantize(("gI", prev), E5M2, staged["gI", prev][:], 0)
-                for s in range(PACK):
-                    dx_matmul(prev, s)
-                for s in range(PACK):
-                    copy_dx_out(prev, s)
-                    if s % 2 == 1:
-                        store_dx(prev, s - 1, s + 1)
-            if g > 0:
-                interleave_gpsimd(g)
-                interleave_scalar(g)
+            quantize(("gT", g), E5M2, staged["gT", g][:], 0)
             if g < last:
-                for t in range(PACK):
-                    if g == 0:
-                        transpose_words(*ahead[t])
-                        copy_words_out(ahead[t][0], ahead[t][2])
-                        if t == 1:
-                            spread_r(nxt)
-                            copy_r_row(nxt)
-                    weigh_dl(g, t)
-                    scale_dl(g, t)
-                    if t + 2 < PACK:
-                        dl_matmul(g, t + 2)
-                    column_sums(g, t)
-                    if t == half:
-                        add_identity(nc.gpsimd, g, 0, half, ident)
-                        round_laplacian(g, 0, half)
-                        if g == 0:
-                            interleave_gpsimd(g)
-                            interleave_scalar(g)
-                    if g > 0 and t + 1 < PACK:
-                        finish_adj(nc.gpsimd, prev, t + 1)
-                        if t % 2 == 0:
-                            store_adj(prev, t, t + 2)
+                spread_r(nxt)
+            dl_matmul(g, 0)
+            dl_matmul(g, 1)
+            for move in ahead:
+                copy_words_out(*move)
+            if g < last:
+                copy_r_row(nxt)
+            quantize(("L", prev), E4M3, staged["L", prev][:], 0)
+            quantize(("gI", prev), E5M2, staged["gI", prev][:], 0)
+            if g == last:
+                break
+            for s in range(PACK):
+                dx_matmul(prev, s, s)
+            for s in range(PACK):
+                copy_dx_out(prev, s)
+                if s % 2 == 1:
+                    store_dx(prev, s - 1, s + 1)
+            open_interleaved(g, "st_gI")
+            interleave_gpsimd(g)
+            interleave_scalar(g, S_COLS)
+            for t in range(PACK):
+                weigh_dl(g, t)
+                scale_dl(g, t)
+                if t + 2 < PACK:
+                    dl_matmul(g, t + 2)
+                column_sums(g, t)
+                if t == HALF:
+                    add_identity(nc.gpsimd, g, 0, HALF, ident)
+                    round_laplacian(g, 0, HALF)
+                if t + 1 < PACK:
+                    finish_adj(nc.gpsimd, prev, t + 1)
+                    if t % 2 == 0:
+                        store_adj(prev, t, t + 2)
 
-        g = last
-        for t in range(1, PACK):
-            finish_adj(nc.gpsimd, g - 1, t)
-            if t % 2 == 1:
-                store_adj(g - 1, t - 1, t + 1)
-        ident_ps = ps_one.tile([P, P], F32, name="r_ps")
-        nc.tensor.transpose(ident_ps[:], ident[:], ident[:])
-        for t in range(half):
-            weigh_dl(g, t)
-            scale_dl(g, t)
-            add_identity(nc.vector, g, t, t + 1, ident_ps)
-            dl_matmul(g, t + 2)
-            column_sums(g, t)
+        g, prev = last, last - 1
+
+        def laplacian_block(t):
+            add_identity(nc.gpsimd, g, t, t + 1, ident)
             round_laplacian(g, t, t + 1)
-        for t in range(half, PACK):
-            weigh_dl(g, t)
-            column_sums(g, t)
-        add_identity(nc.vector, g, half, PACK, ident_ps)
-        round_laplacian(g, half, PACK)
+
+        def dx_block(t, index):
+            quantize(("L", g), E4M3, staged["L", g][:, t * N : (t + 1) * N], t * P)
+            dx_matmul(g, t, index)
+
+        def dx_block_out(k, t, copy=nc.scalar.copy):
+            copy_dx_out(k, t, copy)
+            store_dx(k, t, t + 1)
+
+        def adj_block_out(engine, k, t):
+            finish_adj(engine, k, t)
+            store_adj(k, t, t + 1)
+
+        dx_matmul(prev, 0, 0)
+        dl_matmul(g, 2, R_BANK)
+        dx_matmul(prev, 1, 1)
+        dl_matmul(g, 3, 3)
+        dx_matmul(prev, 2, 2)
+        store_adj(prev, 0, 1)
+        open_interleaved(g, "st_gI_last")
+        interleave_scalar(g, D)
         quantize(("gI", g), E5M2, staged["gI", g][:], 0)
-        quantize(("L", g), E4M3, staged["L", g][:, 0 : half * N], 0)
-        for t in range(half):
-            dx_matmul(g, t)
-            copy_dx_out(g, t)
-            store_dx(g, t, t + 1)
+        degree_term(prev, 1, PACK)
+        finish_adj_scalar(prev, 1)
+        store_adj(prev, 1, 2)
+        adj_block_out(nc.gpsimd, prev, 2)
+        weigh_dl(g, 0)
+        column_sums(g, 0)
+        dx_block_out(prev, 0)
+        dx_matmul(prev, 3, 0)
+        dx_block_out(prev, 1)
+        laplacian_block(0)
+        adj_block_out(nc.gpsimd, prev, 3)
+        weigh_dl(g, 1)
+        column_sums(g, 1)
+        dx_block_out(prev, 2)
+        laplacian_block(1)
+        weigh_dl(g, 2)
+        column_sums(g, 2)
+        dx_block_out(prev, 3)
+        laplacian_block(2)
+        weigh_dl(g, 3)
+        column_sums(g, 3)
+        laplacian_block(3)
+        scale_dl(g, 0)
+        scale_dl(g, 1)
+        dx_block(0, 1)
+        degree_term_vector(g)
+        dx_block(1, 2)
+        adj_block_out(nc.vector, g, 0)
+        adj_block_out(nc.vector, g, 1)
         scale_dl(g, 2)
-        degree_term(g)
-        quantize(("L", g), E4M3, staged["L", g][:, half * N : PACK * N], half * P)
-        for t in range(half, PACK):
-            dx_matmul(g, t)
-        finish_adj(nc.vector, g, 0)
-        store_adj(g, 0, 1)
-        finish_adj(nc.vector, g, 1)
-        store_adj(g, 1, 2)
+        dx_block_out(g, 0)
+        dx_block(2, 0)
+        dx_block(3, DL_BANK)
+        adj_block_out(nc.gpsimd, g, 2)
         scale_dl(g, 3)
-        for t in range(half, PACK):
-            copy_dx_out(g, t)
-            store_dx(g, t, t + 1)
-            finish_adj(nc.vector, g, t)
-            store_adj(g, t, t + 1)
+        dx_block_out(g, 1)
+        dx_block_out(g, 2)
+        adj_block_out(nc.gpsimd, g, 3)
+        dx_block_out(g, 3, nc.vector.tensor_copy)

@@ -19,7 +19,8 @@ P = 128
 PACK = 4
 HALF = PACK // 2
 AHEAD = 3
-S_COLS = 256
+S_COLS = 64
+S_COLS_LAST = 320
 SUM_N = 64
 DL_BANK, R_BANK, SUM_BANK = 4, 6, 7
 
@@ -143,12 +144,12 @@ def tile_cheblayer_pa_v_kernel(tc, x, adj, r, grad_out, out_0, out_1):
 
         def scale_adj(g, t):
             if t == 0:
-                neg_m[g] = work.tile([P, PACK, PACK, P], F32, name="neg_m")
+                neg_m[g] = work.tile([P, 2, PACK, HALF, P], F32, name="neg_m")
             nc.vector.scalar_tensor_tensor(
-                out=neg_m[g][:, t],
-                in0=a_sb[g][:, t, :].rearrange("p (c t) -> p t c", t=PACK),
+                out=neg_m[g][:, :, t],
+                in0=a_sb[g][:, t, :].rearrange("p (c h s) -> p h s c", h=2, s=HALF),
                 scalar=neg_r[:, g, t : t + 1],
-                in1=r_ps[g][:],
+                in1=r_ps[g][:].rearrange("p (h s) c -> p h s c", h=2),
                 op0=ALU.mult,
                 op1=ALU.mult,
             )
@@ -162,30 +163,30 @@ def tile_cheblayer_pa_v_kernel(tc, x, adj, r, grad_out, out_0, out_1):
                 in_=g_sb[g][:, :, 0:cols].rearrange("p t (c i) -> p c t i", i=4),
             )
 
-        def interleave_gpsimd(g):
+        def interleave_gpsimd(g, cols):
             nc.gpsimd.tensor_scalar(
-                out=staged["gI", g][:, PACK * S_COLS : PACK * D].rearrange("p (w t) -> p w t", t=PACK),
-                in0=g_sb[g][:, :, S_COLS:D].rearrange("p t w -> p w t"),
+                out=staged["gI", g][:, PACK * cols : PACK * D].rearrange("p (w t) -> p w t", t=PACK),
+                in0=g_sb[g][:, :, cols:D].rearrange("p t w -> p w t"),
                 scalar1=1.0,
                 scalar2=0.0,
                 op0=ALU.mult,
                 op1=ALU.add,
             )
 
-        def add_identity(engine, g, t0, t1, eye):
-            diag = neg_m[g][:].rearrange("p t s c -> p (t s) c")[:, t0 * (PACK + 1) : (t1 - 1) * (PACK + 1) + 1 : PACK + 1, :]
-            engine.tensor_tensor(
-                out=diag, in0=diag, in1=eye[:].unsqueeze(1).to_broadcast([P, t1 - t0, P]), op=ALU.add
+        def add_identity(g, h):
+            blocks = neg_m[g][:, h].rearrange("p t s c -> p (t s) c")
+            first = HALF * HALF * h
+            diag = blocks[:, first : first + HALF + 2 : HALF + 1, :]
+            nc.gpsimd.tensor_tensor(
+                out=diag, in0=diag, in1=ident[:].unsqueeze(1).to_broadcast([P, HALF, P]), op=ALU.add
             )
 
-        def round_laplacian(g, s0, s1):
-            if s0 == 0:
+        def round_laplacian(g, h):
+            if h == 0:
                 staged["L", g] = stage.tile([P, PACK * N], BF16, name="st_L", align_bytes=64)
             nc.scalar.copy(
-                out=staged["L", g][:, s0 * N : s1 * N].rearrange("p (c i t) -> p c t i", i=4, t=PACK),
-                in_=neg_m[g][:]
-                .rearrange("p t s c -> p t (s c)")[:, :, s0 * P : s1 * P]
-                .rearrange("p t (c i) -> p c t i", i=4),
+                out=staged["L", g][:, h * HALF * N : (h + 1) * HALF * N].rearrange("p (c i t) -> p c t i", i=4, t=PACK),
+                in_=neg_m[g][:, h].rearrange("p t s c -> p t (s c)").rearrange("p t (c i) -> p c t i", i=4),
             )
 
         def weigh_dl(g, t):
@@ -193,10 +194,10 @@ def tile_cheblayer_pa_v_kernel(tc, x, adj, r, grad_out, out_0, out_1):
                 row_sum[g] = stage.tile([P, PACK], F32, name="row_sum")
             q[g, t] = prod.tile([P, N], F32, name="q")
             nc.vector.scalar_tensor_tensor(
-                out=q[g, t][:],
-                in0=dl_ps[g, t][:],
+                out=q[g, t][:].rearrange("p (h w) -> p h w", h=2),
+                in0=dl_ps[g, t][:].rearrange("p (h w) -> p h w", h=2),
                 scalar=1.0,
-                in1=neg_m[g][:, t].rearrange("p s c -> p (s c)"),
+                in1=neg_m[g][:, :, t].rearrange("p h s c -> p h (s c)"),
                 op0=ALU.mult,
                 op1=ALU.mult,
                 accum_out=row_sum[g][:, t : t + 1],
@@ -311,9 +312,9 @@ def tile_cheblayer_pa_v_kernel(tc, x, adj, r, grad_out, out_0, out_1):
                 transpose_words(*ahead[HALF + t])
                 copy_words_out(*ahead[HALF + t])
             if t == HALF:
-                add_identity(nc.gpsimd, 0, 0, HALF, ident)
-                round_laplacian(0, 0, HALF)
-                interleave_gpsimd(0)
+                add_identity(0, 0)
+                round_laplacian(0, 0)
+                interleave_gpsimd(0, S_COLS)
         load(AHEAD)
 
         for g in range(1, B):
@@ -323,58 +324,60 @@ def tile_cheblayer_pa_v_kernel(tc, x, adj, r, grad_out, out_0, out_1):
                 load(g + AHEAD)
             for move in ahead:
                 transpose_words(*move)
-            add_identity(nc.gpsimd, prev, HALF, PACK, ident)
-            degree_term(prev, 0, PACK if g < last else 1)
-            round_laplacian(prev, HALF, PACK)
-            finish_adj(nc.gpsimd, prev, 0)
-            for t in range(PACK):
+            add_identity(prev, 1)
+            round_laplacian(prev, 1)
+            if g == last:
+                break
+            degree_term(prev, 0, PACK)
+            for t in range(PACK - 1):
                 scale_adj(g, t)
             quantize(("xT", g), E4M3, staged["xT", g][:], 0)
             quantize(("gT", g), E5M2, staged["gT", g][:], 0)
-            if g < last:
-                spread_r(nxt)
             dl_matmul(g, 0)
             dl_matmul(g, 1)
+            scale_adj(g, PACK - 1)
+            spread_r(nxt)
             for move in ahead:
                 copy_words_out(*move)
-            if g < last:
-                copy_r_row(nxt)
             quantize(("L", prev), E4M3, staged["L", prev][:], 0)
             quantize(("gI", prev), E5M2, staged["gI", prev][:], 0)
-            if g == last:
-                break
-            for s in range(PACK):
-                dx_matmul(prev, s, s)
+            for t in range(HALF):
+                finish_adj_scalar(prev, t)
+            store_adj(prev, 0, HALF)
+            copy_r_row(nxt)
+            open_interleaved(g, "st_gI")
+            interleave_gpsimd(g, S_COLS)
+            for t in range(HALF):
+                dx_matmul(prev, 2 * t, 2 * t)
+                dx_matmul(prev, 2 * t + 1, 2 * t + 1)
+                weigh_dl(g, t)
+                scale_dl(g, t)
+                dl_matmul(g, t + 2)
             for s in range(PACK):
                 copy_dx_out(prev, s)
                 if s % 2 == 1:
                     store_dx(prev, s - 1, s + 1)
-            open_interleaved(g, "st_gI")
-            interleave_gpsimd(g)
             interleave_scalar(g, S_COLS)
-            for t in range(PACK):
+            finish_adj(nc.gpsimd, prev, 2)
+            add_identity(g, 0)
+            round_laplacian(g, 0)
+            finish_adj(nc.gpsimd, prev, 3)
+            store_adj(prev, HALF, PACK)
+            column_sums(g, 0)
+            column_sums(g, 1)
+            for t in range(HALF, PACK):
                 weigh_dl(g, t)
                 scale_dl(g, t)
-                if t + 2 < PACK:
-                    dl_matmul(g, t + 2)
                 column_sums(g, t)
-                if t == HALF:
-                    add_identity(nc.gpsimd, g, 0, HALF, ident)
-                    round_laplacian(g, 0, HALF)
-                if t + 1 < PACK:
-                    finish_adj(nc.gpsimd, prev, t + 1)
-                    if t % 2 == 0:
-                        store_adj(prev, t, t + 2)
 
         g, prev = last, last - 1
 
-        def laplacian_block(t):
-            add_identity(nc.gpsimd, g, t, t + 1, ident)
-            round_laplacian(g, t, t + 1)
+        def laplacian_half(h):
+            add_identity(g, h)
+            round_laplacian(g, h)
 
-        def dx_block(t, index):
-            quantize(("L", g), E4M3, staged["L", g][:, t * N : (t + 1) * N], t * P)
-            dx_matmul(g, t, index)
+        def quantize_laplacian_half(h):
+            quantize(("L", g), E4M3, staged["L", g][:, h * HALF * N : (h + 1) * HALF * N], h * HALF * P)
 
         def dx_block_out(k, t, copy=nc.scalar.copy):
             copy_dx_out(k, t, copy)
@@ -384,49 +387,55 @@ def tile_cheblayer_pa_v_kernel(tc, x, adj, r, grad_out, out_0, out_1):
             finish_adj(engine, k, t)
             store_adj(k, t, t + 1)
 
-        dx_matmul(prev, 0, 0)
-        dl_matmul(g, 2, R_BANK)
-        dx_matmul(prev, 1, 1)
-        dl_matmul(g, 3, 3)
-        dx_matmul(prev, 2, 2)
-        store_adj(prev, 0, 1)
         open_interleaved(g, "st_gI_last")
-        interleave_scalar(g, D)
+        interleave_gpsimd(g, S_COLS_LAST)
+        interleave_scalar(g, S_COLS_LAST)
+        degree_term(prev, 0, PACK)
+        for t in range(PACK):
+            finish_adj_scalar(prev, t)
+            store_adj(prev, t, t + 1)
+        for t in range(PACK):
+            scale_adj(g, t)
+        quantize(("xT", g), E4M3, staged["xT", g][:], 0)
+        quantize(("gT", g), E5M2, staged["gT", g][:], 0)
+        dl_matmul(g, 0)
+        dl_matmul(g, 1)
+        dl_matmul(g, 2, R_BANK)
+        dl_matmul(g, 3, 3)
+        quantize(("L", prev), E4M3, staged["L", prev][:], 0)
+        quantize(("gI", prev), E5M2, staged["gI", prev][:], 0)
+        for s in range(PACK - 1):
+            dx_matmul(prev, s, s)
         quantize(("gI", g), E5M2, staged["gI", g][:], 0)
-        degree_term(prev, 1, PACK)
-        finish_adj_scalar(prev, 1)
-        store_adj(prev, 1, 2)
-        adj_block_out(nc.gpsimd, prev, 2)
         weigh_dl(g, 0)
         column_sums(g, 0)
         dx_block_out(prev, 0)
         dx_matmul(prev, 3, 0)
         dx_block_out(prev, 1)
-        laplacian_block(0)
-        adj_block_out(nc.gpsimd, prev, 3)
         weigh_dl(g, 1)
         column_sums(g, 1)
         dx_block_out(prev, 2)
-        laplacian_block(1)
+        laplacian_half(0)
         weigh_dl(g, 2)
         column_sums(g, 2)
         dx_block_out(prev, 3)
-        laplacian_block(2)
         weigh_dl(g, 3)
         column_sums(g, 3)
-        laplacian_block(3)
+        laplacian_half(1)
         scale_dl(g, 0)
         scale_dl(g, 1)
-        dx_block(0, 1)
+        quantize_laplacian_half(0)
+        dx_matmul(g, 0, 1)
+        dx_matmul(g, 1, 2)
         degree_term_vector(g)
-        dx_block(1, 2)
+        scale_dl(g, 2)
         adj_block_out(nc.vector, g, 0)
         adj_block_out(nc.vector, g, 1)
-        scale_dl(g, 2)
         dx_block_out(g, 0)
-        dx_block(2, 0)
-        dx_block(3, DL_BANK)
-        adj_block_out(nc.gpsimd, g, 2)
+        quantize_laplacian_half(1)
+        dx_matmul(g, 2, 0)
+        dx_matmul(g, 3, DL_BANK)
+        adj_block_out(nc.vector, g, 2)
         scale_dl(g, 3)
         dx_block_out(g, 1)
         dx_block_out(g, 2)

@@ -18,10 +18,11 @@ ACT = mybir.ActivationFunctionType
 P = 128
 PACK = 4
 HALF = PACK // 2
+RUN = 4
 AHEAD = 3
-S_COLS = 64
-S_COLS_LAST = 320
-SUM_N = 64
+SCALAR_COLS = 64
+SCALAR_COLS_LAST = 320
+SUM_WIDTH = 64
 DL_BANK, R_BANK, SUM_BANK = 4, 6, 7
 
 
@@ -33,15 +34,16 @@ def tile_cheblayer_pa_v_kernel(tc, x, adj, r, grad_out, out_0, out_1):
         inp = ctx.enter_context(tc.tile_pool(name="inp", bufs=AHEAD + 2))
         work = ctx.enter_context(tc.tile_pool(name="work", bufs=3))
         stage = ctx.enter_context(tc.tile_pool(name="stage", bufs=2))
-        prod = ctx.enter_context(tc.tile_pool(name="prod", bufs=4))
+        prod = ctx.enter_context(tc.tile_pool(name="prod", bufs=PACK))
         psum = ctx.enter_context(tc.psum_pool(name="psum", bufs=1))
         ctx.enter_context(tc.manual_schedule())
 
-        a_sb, g_sb, x_sb, banks, staged, quant = {}, {}, {}, {}, {}, {}
-        r_ps, r_row, neg_m, dl_ps, dl_r, q, row_sum, sum_ps, dd, dx = {}, {}, {}, {}, {}, {}, {}, {}, {}, {}
+        a_sb, g_sb, x_sb, moved, staged, quant = {}, {}, {}, {}, {}, {}
+        r_ps, r_row, neg_m, dl_ps, weighed, row_sum, sum_ps, dd = {}, {}, {}, {}, {}, {}, {}, {}
+        d_adj, dx_ps, dx_sb = {}, {}, {}
 
-        def open_bank(index, shape):
-            return psum.tile(shape, F32, name="bank%d" % index)
+        def open_bank(bank, shape):
+            return psum.tile(shape, F32, name="bank%d" % bank)
 
         def rows(hbm, g):
             return hbm[g].rearrange("(p t) w -> p t w", t=PACK)
@@ -75,12 +77,12 @@ def tile_cheblayer_pa_v_kernel(tc, x, adj, r, grad_out, out_0, out_1):
 
         ident = const.tile([P, P], F32, name="ident")
         make_identity(nc, ident[:])
-        ones = const.tile([P, SUM_N], F32, name="ones")
+        ones = const.tile([P, SUM_WIDTH], F32, name="ones")
         nc.vector.memset(ones[:], 1.0)
         neg_r = const.tile([P, B, PACK], F32, name="neg_r")
         dd_gain = const.tile([P, B, PACK], F32, name="dd_gain")
 
-        def degree_constants(r_col, graphs):
+        def node_constants(r_col, graphs):
             nc.scalar.activation(out=neg_r[:, graphs, :], in_=r_col[:], func=ACT.Copy, scale=-1.0)
             nc.vector.scalar_tensor_tensor(
                 out=dd_gain[:, graphs, :],
@@ -91,56 +93,70 @@ def tile_cheblayer_pa_v_kernel(tc, x, adj, r, grad_out, out_0, out_1):
                 op1=ALU.mult,
             )
 
-        def transpose_words(key, src, h, index):
-            bank = open_bank(index, [P, 2, 2, P])
-            for tt in range(2):
-                words = src[:, 2 * h + tt, :].bitcast(F32)
-                for u in range(2):
-                    nc.tensor.transpose(bank[:, tt, u, :], words[:, u : D // 2 : 2], ident[:])
-            banks[key, h] = bank
 
-        def copy_words_out(key, src, h, index):
+        def moves(g):
+            halves = [((kind, g), tiles[g], h) for kind, tiles in (("xT", x_sb), ("gT", g_sb)) for h in range(2)]
+            return [half + (bank,) for bank, half in enumerate(halves)]
+
+        def transpose_pairs(move):
+            key, src, h, bank = move
+            moved[key, h] = open_bank(bank, [P, HALF, 2, P])
+            for slot in range(HALF):
+                pairs = src[:, HALF * h + slot, :].bitcast(F32)
+                for u in range(2):
+                    nc.tensor.transpose(moved[key, h][:, slot, u, :], pairs[:, u : D // 2 : 2], ident[:])
+
+        def copy_pairs_out(move):
+            key, h = move[0], move[2]
             if h == 0:
                 staged[key] = stage.tile([P, PACK * N], BF16, name="st_" + key[0], align_bytes=64)
-            words = staged[key][:].bitcast(F32).rearrange("p (h t c u) -> p h t c u", h=2, t=2, u=2)
-            nc.scalar.copy(out=words[:, h], in_=banks[key, h][:].rearrange("p t u c -> p t c u"))
+            pairs = staged[key][:].bitcast(F32).rearrange("p (h t c u) -> p h t c u", h=2, t=HALF, u=2)
+            nc.scalar.copy(out=pairs[:, h], in_=moved[key, h][:].rearrange("p t u c -> p t c u"))
 
-        def quantize(key, fmt, src, first):
-            if first == 0:
+
+        def quantize(key, fmt, c0=0, c1=N):
+            if c0 == 0:
                 codes = stage.tile([P, N], U32, name="codes_" + key[0], align_bytes=64)
                 scales = stage.tile([P, N], U8, name="scales_" + key[0], align_bytes=64)
                 quant[key] = (codes, scales, fmt)
-            codes, scales, fmt = quant[key]
-            cols = slice(first, first + src.shape[1] // PACK)
-            nc.vector.quantize_mx(out=codes[:, cols].bitcast(fmt), scales=scales[:, cols], in_=src)
+            codes, scales = quant[key][:2]
+            nc.vector.quantize_mx(
+                out=codes[:, c0:c1].bitcast(fmt), scales=scales[:, c0:c1], in_=staged[key][:, PACK * c0 : PACK * c1]
+            )
 
-        def mx_pass(acc, lhs_key, t, rhs_key):
-            lc, ls, lf = quant[lhs_key]
-            rc, rs, rf = quant[rhs_key]
-            cols = slice(t * P, (t + 1) * P)
+        def mx_pass(acc, lhs_key, block, rhs_key):
+            lhs_codes, lhs_scales, lhs_fmt = quant[lhs_key]
+            rhs_codes, rhs_scales, rhs_fmt = quant[rhs_key]
+            cols = slice(block * P, (block + 1) * P)
             nc.tensor.matmul_mx(
                 out=acc[:],
-                lhsT=lc[:, cols].bitcast(lf),
-                lhsT_scale=ls[:, cols],
-                rhs=rc[:].bitcast(rf),
-                rhs_scale=rs[:],
+                lhsT=lhs_codes[:, cols].bitcast(lhs_fmt),
+                lhsT_scale=lhs_scales[:, cols],
+                rhs=rhs_codes[:].bitcast(rhs_fmt),
+                rhs_scale=rhs_scales[:],
                 start=True,
                 stop=True,
             )
 
-        def dl_matmul(g, t, index=None):
-            dl_ps[g, t] = open_bank(DL_BANK + t % 2 if index is None else index, [P, N])
+        def dl_matmul(g, t, bank):
+            dl_ps[g, t] = open_bank(bank, [P, N])
             mx_pass(dl_ps[g, t], ("gT", g), t, ("xT", g))
+
+        def dx_matmul(g, s, bank):
+            dx_ps[g, s] = open_bank(bank, [P, D])
+            mx_pass(dx_ps[g, s], ("L", g), s, ("gI", g))
+
 
         def spread_r(g):
             r_ps[g] = open_bank(R_BANK, [P, PACK, P])
             r_col = r_first[:, 0, :] if g == 0 else r_rest[:, g - 1, :]
-            for t in range(PACK):
-                nc.tensor.transpose(r_ps[g][:, t, :], r_col[:, t : t + 1].to_broadcast([P, P]), ident[:])
+            for s in range(PACK):
+                nc.tensor.transpose(r_ps[g][:, s, :], r_col[:, s : s + 1].to_broadcast([P, P]), ident[:])
 
         def copy_r_row(g):
             r_row[g] = stage.tile([P, P, PACK], F32, name="r_row")
-            nc.scalar.copy(out=r_row[g][:], in_=r_ps[g][:].rearrange("p t c -> p c t"))
+            nc.scalar.copy(out=r_row[g][:], in_=r_ps[g][:].rearrange("p s c -> p c s"))
+
 
         def scale_adj(g, t):
             if t == 0:
@@ -154,13 +170,29 @@ def tile_cheblayer_pa_v_kernel(tc, x, adj, r, grad_out, out_0, out_1):
                 op1=ALU.mult,
             )
 
+        def form_laplacian(g, h):
+            blocks = neg_m[g][:, h].rearrange("p t s c -> p (t s) c")
+            first = HALF * HALF * h
+            diagonal = blocks[:, first : first + HALF + 2 : HALF + 1, :]
+            nc.gpsimd.tensor_tensor(
+                out=diagonal, in0=diagonal, in1=ident[:].unsqueeze(1).to_broadcast([P, HALF, P]), op=ALU.add
+            )
+            if h == 0:
+                staged["L", g] = stage.tile([P, PACK * N], BF16, name="st_L", align_bytes=64)
+            half_out = staged["L", g][:, h * HALF * N : (h + 1) * HALF * N]
+            nc.scalar.copy(
+                out=half_out.rearrange("p (c i t) -> p c t i", i=RUN, t=PACK),
+                in_=neg_m[g][:, h].rearrange("p t s c -> p t (s c)").rearrange("p t (c i) -> p c t i", i=RUN),
+            )
+
+
         def open_interleaved(g, name):
             staged["gI", g] = stage.tile([P, PACK * D], BF16, name=name, bufs=1, align_bytes=64)
 
         def interleave_scalar(g, cols):
             nc.scalar.copy(
-                out=staged["gI", g][:, 0 : PACK * cols].rearrange("p (c i t) -> p c t i", i=4, t=PACK),
-                in_=g_sb[g][:, :, 0:cols].rearrange("p t (c i) -> p c t i", i=4),
+                out=staged["gI", g][:, 0 : PACK * cols].rearrange("p (c i t) -> p c t i", i=RUN, t=PACK),
+                in_=g_sb[g][:, :, 0:cols].rearrange("p t (c i) -> p c t i", i=RUN),
             )
 
         def interleave_gpsimd(g, cols):
@@ -173,28 +205,13 @@ def tile_cheblayer_pa_v_kernel(tc, x, adj, r, grad_out, out_0, out_1):
                 op1=ALU.add,
             )
 
-        def add_identity(g, h):
-            blocks = neg_m[g][:, h].rearrange("p t s c -> p (t s) c")
-            first = HALF * HALF * h
-            diag = blocks[:, first : first + HALF + 2 : HALF + 1, :]
-            nc.gpsimd.tensor_tensor(
-                out=diag, in0=diag, in1=ident[:].unsqueeze(1).to_broadcast([P, HALF, P]), op=ALU.add
-            )
-
-        def round_laplacian(g, h):
-            if h == 0:
-                staged["L", g] = stage.tile([P, PACK * N], BF16, name="st_L", align_bytes=64)
-            nc.scalar.copy(
-                out=staged["L", g][:, h * HALF * N : (h + 1) * HALF * N].rearrange("p (c i t) -> p c t i", i=4, t=PACK),
-                in_=neg_m[g][:, h].rearrange("p t s c -> p t (s c)").rearrange("p t (c i) -> p c t i", i=4),
-            )
 
         def weigh_dl(g, t):
             if t == 0:
                 row_sum[g] = stage.tile([P, PACK], F32, name="row_sum")
-            q[g, t] = prod.tile([P, N], F32, name="q")
+            weighed[g, t] = prod.tile([P, N], F32, name="weighed")
             nc.vector.scalar_tensor_tensor(
-                out=q[g, t][:].rearrange("p (h w) -> p h w", h=2),
+                out=weighed[g, t][:].rearrange("p (h w) -> p h w", h=2),
                 in0=dl_ps[g, t][:].rearrange("p (h w) -> p h w", h=2),
                 scalar=1.0,
                 in1=neg_m[g][:, :, t].rearrange("p h s c -> p h (s c)"),
@@ -205,9 +222,9 @@ def tile_cheblayer_pa_v_kernel(tc, x, adj, r, grad_out, out_0, out_1):
 
         def scale_dl(g, t):
             if t == 0:
-                dl_r[g] = work.tile([P, PACK, N], F32, name="dl_r")
+                d_adj[g] = work.tile([P, PACK, N], F32, name="d_adj")
             nc.vector.tensor_tensor(
-                out=dl_r[g][:, t, :].rearrange("p (c s) -> p c s", s=PACK),
+                out=d_adj[g][:, t, :].rearrange("p (c s) -> p c s", s=PACK),
                 in0=dl_ps[g, t][:].rearrange("p (s c) -> p c s", s=PACK),
                 in1=r_row[g][:],
                 op=ALU.mult,
@@ -215,11 +232,11 @@ def tile_cheblayer_pa_v_kernel(tc, x, adj, r, grad_out, out_0, out_1):
 
         def column_sums(g, t):
             if t == 0:
-                sum_ps[g] = open_bank(SUM_BANK, [P, PACK, SUM_N])
+                sum_ps[g] = open_bank(SUM_BANK, [P, PACK, SUM_WIDTH])
             for s in range(PACK):
                 nc.tensor.matmul(
                     sum_ps[g][:, s, :],
-                    lhsT=q[g, t][:, s * P : (s + 1) * P],
+                    lhsT=weighed[g, t][:, s * P : (s + 1) * P],
                     rhs=ones[:],
                     start=(t == 0 and s == 0),
                     stop=False,
@@ -227,10 +244,9 @@ def tile_cheblayer_pa_v_kernel(tc, x, adj, r, grad_out, out_0, out_1):
             if t == PACK - 1:
                 nc.tensor.matmul(sum_ps[g][:, :, 0], lhsT=ident[:], rhs=row_sum[g][:], start=False, stop=True)
 
-        def degree_term(g, t0, t1):
-            if t0 == 0:
-                dd[g] = stage.tile([P, PACK], F32, name="dd")
-            for t in range(t0, t1):
+        def degree_term_scalar(g):
+            dd[g] = stage.tile([P, PACK], F32, name="dd")
+            for t in range(PACK):
                 nc.scalar.activation(
                     out=dd[g][:, t : t + 1], in_=sum_ps[g][:, t, 0:1], func=ACT.Copy, scale=dd_gain[:, g, t : t + 1]
                 )
@@ -241,8 +257,8 @@ def tile_cheblayer_pa_v_kernel(tc, x, adj, r, grad_out, out_0, out_1):
 
         def finish_adj_scalar(g, t):
             nc.scalar.activation(
-                out=dl_r[g][:, t, :],
-                in_=dl_r[g][:, t, :],
+                out=d_adj[g][:, t, :],
+                in_=d_adj[g][:, t, :],
                 func=ACT.Identity,
                 scale=neg_r[:, g, t : t + 1],
                 bias=dd[g][:, t : t + 1],
@@ -250,8 +266,8 @@ def tile_cheblayer_pa_v_kernel(tc, x, adj, r, grad_out, out_0, out_1):
 
         def finish_adj(engine, g, t):
             engine.tensor_scalar(
-                out=dl_r[g][:, t, :],
-                in0=dl_r[g][:, t, :],
+                out=d_adj[g][:, t, :],
+                in0=d_adj[g][:, t, :],
                 scalar1=neg_r[:, g, t : t + 1],
                 scalar2=dd[g][:, t : t + 1],
                 op0=ALU.mult,
@@ -259,185 +275,167 @@ def tile_cheblayer_pa_v_kernel(tc, x, adj, r, grad_out, out_0, out_1):
             )
 
         def store_adj(g, t0, t1):
-            nc.sync.dma_start(out=rows(out_1, g)[:, t0:t1, :], in_=dl_r[g][:, t0:t1, :])
+            nc.sync.dma_start(out=rows(out_1, g)[:, t0:t1, :], in_=d_adj[g][:, t0:t1, :])
 
-        def dx_matmul(g, s, index):
-            banks["dx", g, s] = open_bank(index, [P, D])
-            mx_pass(banks["dx", g, s], ("L", g), s, ("gI", g))
-
-        def copy_dx_out(g, s, copy=nc.scalar.copy):
+        def copy_dx_out(copy, g, s):
             if s == 0:
-                dx[g] = work.tile([P, PACK, D], F32, name="dx")
-            copy(out=dx[g][:, s, :], in_=banks["dx", g, s][:])
+                dx_sb[g] = work.tile([P, PACK, D], F32, name="dx_sb")
+            copy(out=dx_sb[g][:, s, :], in_=dx_ps[g, s][:])
 
         def store_dx(g, s0, s1):
-            nc.sync.dma_start(out=rows(out_0, g)[:, s0:s1, :], in_=dx[g][:, s0:s1, :])
+            nc.sync.dma_start(out=rows(out_0, g)[:, s0:s1, :], in_=dx_sb[g][:, s0:s1, :])
 
-        def moves(g):
-            halves = [((name, g), src[g], h) for name, src in (("xT", x_sb), ("gT", g_sb)) for h in range(2)]
-            return [half + (index,) for index, half in enumerate(halves)]
-
-        last = B - 1
-
-        degree_constants(r_first, slice(0, 1))
+        node_constants(r_first, slice(0, 1))
         spread_r(0)
         for move in moves(0):
-            transpose_words(*move)
-            copy_words_out(*move)
+            transpose_pairs(move)
+            copy_pairs_out(move)
         for t in range(PACK - 1):
             scale_adj(0, t)
-        quantize(("xT", 0), E4M3, staged["xT", 0][:], 0)
-        quantize(("gT", 0), E5M2, staged["gT", 0][:, 0 : HALF * N], 0)
-        dl_matmul(0, 0)
-        dl_matmul(0, 1)
+        quantize(("xT", 0), E4M3)
+        quantize(("gT", 0), E5M2, 0, HALF * P)
+        for t in range(HALF):
+            dl_matmul(0, t, DL_BANK + t)
         scale_adj(0, PACK - 1)
         copy_r_row(0)
-        quantize(("gT", 0), E5M2, staged["gT", 0][:, HALF * N : PACK * N], HALF * P)
-        degree_constants(r_rest, slice(1, B))
+        quantize(("gT", 0), E5M2, HALF * P, N)
+        node_constants(r_rest, slice(1, B))
         open_interleaved(0, "st_gI")
-        interleave_scalar(0, S_COLS)
-        ahead = moves(1)
-        for move in ahead[:HALF]:
-            transpose_words(*move)
-            copy_words_out(*move)
+        interleave_scalar(0, SCALAR_COLS)
         spread_r(1)
         copy_r_row(1)
+        catch_up = moves(1) + moves(2)
         for t in range(PACK):
             weigh_dl(0, t)
             scale_dl(0, t)
-            if t + 2 < PACK:
-                dl_matmul(0, t + 2)
-            column_sums(0, t)
             if t < HALF:
-                transpose_words(*ahead[HALF + t])
-                copy_words_out(*ahead[HALF + t])
-            if t == HALF:
-                add_identity(0, 0)
-                round_laplacian(0, 0)
-                interleave_gpsimd(0, S_COLS)
+                dl_matmul(0, t + HALF, DL_BANK + t)
+            if t > 0:
+                for move in catch_up[HALF * (t - 1) : HALF * t]:
+                    transpose_pairs(move)
+            column_sums(0, t)
+            if t == HALF - 1:
+                form_laplacian(0, 0)
+                interleave_gpsimd(0, SCALAR_COLS)
+            if 0 < t <= HALF:
+                for move in catch_up[HALF * (t - 1) : HALF * t]:
+                    copy_pairs_out(move)
         load(AHEAD)
 
-        for g in range(1, B):
+        last = B - 1
+        for g in range(1, last):
             prev, nxt = g - 1, g + 1
-            ahead = moves(nxt) if g < last else []
             if g + AHEAD < B:
                 load(g + AHEAD)
-            for move in ahead:
-                transpose_words(*move)
-            add_identity(prev, 1)
-            round_laplacian(prev, 1)
-            if g == last:
-                break
-            degree_term(prev, 0, PACK)
+            form_laplacian(prev, 1)
             for t in range(PACK - 1):
                 scale_adj(g, t)
-            quantize(("xT", g), E4M3, staged["xT", g][:], 0)
-            quantize(("gT", g), E5M2, staged["gT", g][:], 0)
-            dl_matmul(g, 0)
-            dl_matmul(g, 1)
+            quantize(("xT", g), E4M3)
+            quantize(("gT", g), E5M2)
+            for t in range(HALF):
+                dl_matmul(g, t, DL_BANK + t)
+            if g == 1:
+                for move in catch_up[PACK + HALF :]:
+                    transpose_pairs(move)
             scale_adj(g, PACK - 1)
             spread_r(nxt)
-            for move in ahead:
-                copy_words_out(*move)
-            quantize(("L", prev), E4M3, staged["L", prev][:], 0)
-            quantize(("gI", prev), E5M2, staged["gI", prev][:], 0)
+            for move in moves(nxt)[:HALF]:
+                copy_pairs_out(move)
+            degree_term_scalar(prev)
+            for move in moves(nxt)[HALF:]:
+                copy_pairs_out(move)
+            quantize(("L", prev), E4M3)
+            quantize(("gI", prev), E5M2)
+            for s in range(PACK):
+                dx_matmul(prev, s, s)
             for t in range(HALF):
                 finish_adj_scalar(prev, t)
             store_adj(prev, 0, HALF)
             copy_r_row(nxt)
+            for h in range(2):
+                for s in range(HALF * h, HALF * (h + 1)):
+                    copy_dx_out(nc.scalar.copy, prev, s)
+                store_dx(prev, HALF * h, HALF * (h + 1))
             open_interleaved(g, "st_gI")
-            interleave_gpsimd(g, S_COLS)
+            interleave_gpsimd(g, SCALAR_COLS)
+            interleave_scalar(g, SCALAR_COLS)
             for t in range(HALF):
-                dx_matmul(prev, 2 * t, 2 * t)
-                dx_matmul(prev, 2 * t + 1, 2 * t + 1)
                 weigh_dl(g, t)
                 scale_dl(g, t)
-                dl_matmul(g, t + 2)
-            for s in range(PACK):
-                copy_dx_out(prev, s)
-                if s % 2 == 1:
-                    store_dx(prev, s - 1, s + 1)
-            interleave_scalar(g, S_COLS)
-            finish_adj(nc.gpsimd, prev, 2)
-            add_identity(g, 0)
-            round_laplacian(g, 0)
-            finish_adj(nc.gpsimd, prev, 3)
-            store_adj(prev, HALF, PACK)
-            column_sums(g, 0)
-            column_sums(g, 1)
-            for t in range(HALF, PACK):
-                weigh_dl(g, t)
-                scale_dl(g, t)
+                dl_matmul(g, t + HALF, DL_BANK + t)
                 column_sums(g, t)
+                if t == HALF - 1:
+                    form_laplacian(g, 0)
+                finish_adj(nc.gpsimd, prev, t + HALF)
+            store_adj(prev, HALF, PACK)
+            for h in range(2):
+                weigh_dl(g, HALF + h)
+                scale_dl(g, HALF + h)
+                if g + 2 < B:
+                    for move in moves(g + 2)[HALF * h : HALF * (h + 1)]:
+                        transpose_pairs(move)
+                column_sums(g, HALF + h)
 
         g, prev = last, last - 1
 
-        def laplacian_half(h):
-            add_identity(g, h)
-            round_laplacian(g, h)
+        def dx_block_out(copy, graph, s):
+            copy_dx_out(copy, graph, s)
+            store_dx(graph, s, s + 1)
 
-        def quantize_laplacian_half(h):
-            quantize(("L", g), E4M3, staged["L", g][:, h * HALF * N : (h + 1) * HALF * N], h * HALF * P)
+        def adj_slot_out(engine, t):
+            finish_adj(engine, g, t)
+            store_adj(g, t, t + 1)
 
-        def dx_block_out(k, t, copy=nc.scalar.copy):
-            copy_dx_out(k, t, copy)
-            store_dx(k, t, t + 1)
+        def dx_half(h, banks):
+            quantize(("L", g), E4M3, h * HALF * P, (h + 1) * HALF * P)
+            for s, bank in enumerate(banks):
+                dx_matmul(g, HALF * h + s, bank)
 
-        def adj_block_out(engine, k, t):
-            finish_adj(engine, k, t)
-            store_adj(k, t, t + 1)
-
+        form_laplacian(prev, 1)
         open_interleaved(g, "st_gI_last")
-        interleave_gpsimd(g, S_COLS_LAST)
-        interleave_scalar(g, S_COLS_LAST)
-        degree_term(prev, 0, PACK)
+        interleave_gpsimd(g, SCALAR_COLS_LAST)
+        degree_term_scalar(prev)
         for t in range(PACK):
             finish_adj_scalar(prev, t)
             store_adj(prev, t, t + 1)
+        interleave_scalar(g, SCALAR_COLS_LAST)
         for t in range(PACK):
             scale_adj(g, t)
-        quantize(("xT", g), E4M3, staged["xT", g][:], 0)
-        quantize(("gT", g), E5M2, staged["gT", g][:], 0)
-        dl_matmul(g, 0)
-        dl_matmul(g, 1)
-        dl_matmul(g, 2, R_BANK)
-        dl_matmul(g, 3, 3)
-        quantize(("L", prev), E4M3, staged["L", prev][:], 0)
-        quantize(("gI", prev), E5M2, staged["gI", prev][:], 0)
+        quantize(("xT", g), E4M3)
+        quantize(("gT", g), E5M2)
+        for t, bank in enumerate((DL_BANK, DL_BANK + 1, R_BANK, PACK - 1)):
+            dl_matmul(g, t, bank)
+        quantize(("L", prev), E4M3)
+        quantize(("gI", prev), E5M2)
         for s in range(PACK - 1):
             dx_matmul(prev, s, s)
-        quantize(("gI", g), E5M2, staged["gI", g][:], 0)
         weigh_dl(g, 0)
         column_sums(g, 0)
-        dx_block_out(prev, 0)
-        dx_matmul(prev, 3, 0)
-        dx_block_out(prev, 1)
-        weigh_dl(g, 1)
-        column_sums(g, 1)
-        dx_block_out(prev, 2)
-        laplacian_half(0)
-        weigh_dl(g, 2)
-        column_sums(g, 2)
-        dx_block_out(prev, 3)
-        weigh_dl(g, 3)
-        column_sums(g, 3)
-        laplacian_half(1)
-        scale_dl(g, 0)
-        scale_dl(g, 1)
-        quantize_laplacian_half(0)
-        dx_matmul(g, 0, 1)
-        dx_matmul(g, 1, 2)
+        dx_block_out(nc.scalar.copy, prev, 0)
+        dx_matmul(prev, PACK - 1, 0)
+        for t in range(1, PACK):
+            dx_block_out(nc.scalar.copy, prev, t)
+            if t == HALF:
+                form_laplacian(g, 0)
+            if t < PACK - 1:
+                weigh_dl(g, t)
+                column_sums(g, t)
+        weigh_dl(g, PACK - 1)
+        column_sums(g, PACK - 1)
+        form_laplacian(g, 1)
+        for t in range(HALF):
+            scale_dl(g, t)
+        quantize(("gI", g), E5M2)
+        dx_half(0, (1, 2))
         degree_term_vector(g)
-        scale_dl(g, 2)
-        adj_block_out(nc.vector, g, 0)
-        adj_block_out(nc.vector, g, 1)
-        dx_block_out(g, 0)
-        quantize_laplacian_half(1)
-        dx_matmul(g, 2, 0)
-        dx_matmul(g, 3, DL_BANK)
-        adj_block_out(nc.vector, g, 2)
-        scale_dl(g, 3)
-        dx_block_out(g, 1)
-        dx_block_out(g, 2)
-        adj_block_out(nc.gpsimd, g, 3)
-        dx_block_out(g, 3, nc.vector.tensor_copy)
+        scale_dl(g, HALF)
+        for t in range(HALF):
+            adj_slot_out(nc.vector, t)
+        dx_block_out(nc.scalar.copy, g, 0)
+        dx_half(1, (0, DL_BANK))
+        adj_slot_out(nc.vector, HALF)
+        scale_dl(g, PACK - 1)
+        for s in range(1, PACK - 1):
+            dx_block_out(nc.scalar.copy, g, s)
+        adj_slot_out(nc.gpsimd, PACK - 1)
+        dx_block_out(nc.vector.tensor_copy, g, PACK - 1)

from contextlib import ExitStack

import concourse.mybir as mybir
from concourse.masks import make_identity

B, N, D = 8, 512, 512
FLOPS = 2 * 2 * B * N * N * D

F32 = mybir.dt.float32
BF16 = mybir.dt.bfloat16
U32 = mybir.dt.uint32
U8 = mybir.dt.uint8
E4M3 = mybir.dt.float8_e4m3fn_x4
E5M2 = mybir.dt.float8_e5m2_x4
ALU = mybir.AluOpType
ACT = mybir.ActivationFunctionType

P = 128
PACK = 4
HALF = PACK // 2
RUN = 4
AHEAD = 3
SCALAR_COLS = 64
SCALAR_COLS_LAST = 320
SUM_WIDTH = 64
DL_BANK, R_BANK, SUM_BANK = 4, 6, 7


def tile_cheblayer_pa_v_kernel(tc, x, adj, r, grad_out, out_0, out_1):
    nc = tc.nc

    with ExitStack() as ctx:
        const = ctx.enter_context(tc.tile_pool(name="const", bufs=1))
        inp = ctx.enter_context(tc.tile_pool(name="inp", bufs=AHEAD + 2))
        work = ctx.enter_context(tc.tile_pool(name="work", bufs=3))
        stage = ctx.enter_context(tc.tile_pool(name="stage", bufs=2))
        prod = ctx.enter_context(tc.tile_pool(name="prod", bufs=PACK))
        psum = ctx.enter_context(tc.psum_pool(name="psum", bufs=1))
        ctx.enter_context(tc.manual_schedule())

        a_sb, g_sb, x_sb, moved, staged, quant = {}, {}, {}, {}, {}, {}
        r_ps, r_row, neg_m, dl_ps, weighed, row_sum, sum_ps, dd = {}, {}, {}, {}, {}, {}, {}, {}
        d_adj, dx_ps, dx_sb = {}, {}, {}

        def open_bank(bank, shape):
            return psum.tile(shape, F32, name="bank%d" % bank)

        def rows(hbm, g):
            return hbm[g].rearrange("(p t) w -> p t w", t=PACK)

        def open_rows(name):
            flat = inp.tile([P, PACK * D], BF16, name=name, align_bytes=64)
            return flat[:].rearrange("p (t w) -> p t w", t=PACK)

        def load_rows(dst, hbm, g, t0, t1):
            nc.sync.dma_start(out=dst[:, t0:t1, :], in_=rows(hbm, g)[:, t0:t1, :])

        def load(g):
            for tiles, hbm, name in ((x_sb, x, "x_sb"), (g_sb, grad_out, "g_sb"), (a_sb, adj, "a_sb")):
                tiles[g] = open_rows(name)
                load_rows(tiles[g], hbm, g, 0, PACK)

        r_first = const.tile([P, 1, PACK], F32, name="r_first")
        r_rest = const.tile([P, B - 1, PACK], F32, name="r_rest")
        r_hbm = r.rearrange("g (p t) -> p g t", t=PACK)
        nc.sync.dma_start(out=r_first[:], in_=r_hbm[:, 0:1, :])
        x_sb[0], g_sb[0], a_sb[0] = open_rows("x_sb"), open_rows("g_sb"), open_rows("a_sb")
        load_rows(a_sb[0], adj, 0, 0, HALF)
        load_rows(x_sb[0], x, 0, 0, HALF)
        load_rows(x_sb[0], x, 0, HALF, PACK)
        load_rows(g_sb[0], grad_out, 0, 0, HALF)
        load_rows(a_sb[0], adj, 0, HALF, PACK)
        load_rows(g_sb[0], grad_out, 0, HALF, PACK)
        nc.sync.dma_start(out=r_rest[:], in_=r_hbm[:, 1:B, :])
        for g in range(1, AHEAD):
            load(g)

        ident = const.tile([P, P], F32, name="ident")
        make_identity(nc, ident[:])
        ones = const.tile([P, SUM_WIDTH], F32, name="ones")
        nc.vector.memset(ones[:], 1.0)
        neg_r = const.tile([P, B, PACK], F32, name="neg_r")
        dd_gain = const.tile([P, B, PACK], F32, name="dd_gain")

        def node_constants(r_col, graphs):
            nc.scalar.activation(out=neg_r[:, graphs, :], in_=r_col[:], func=ACT.Copy, scale=-1.0)
            nc.vector.scalar_tensor_tensor(
                out=dd_gain[:, graphs, :],
                in0=r_col[:],
                scalar=-0.5,
                in1=r_col[:],
                op0=ALU.mult,
                op1=ALU.mult,
            )


        def moves(g):
            halves = [((kind, g), tiles[g], h) for kind, tiles in (("xT", x_sb), ("gT", g_sb)) for h in range(2)]
            return [half + (bank,) for bank, half in enumerate(halves)]

        def transpose_pairs(move):
            key, src, h, bank = move
            moved[key, h] = open_bank(bank, [P, HALF, 2, P])
            for slot in range(HALF):
                pairs = src[:, HALF * h + slot, :].bitcast(F32)
                for u in range(2):
                    nc.tensor.transpose(moved[key, h][:, slot, u, :], pairs[:, u : D // 2 : 2], ident[:])

        def copy_pairs_out(move):
            key, h = move[0], move[2]
            if h == 0:
                staged[key] = stage.tile([P, PACK * N], BF16, name="st_" + key[0], align_bytes=64)
            pairs = staged[key][:].bitcast(F32).rearrange("p (h t c u) -> p h t c u", h=2, t=HALF, u=2)
            nc.scalar.copy(out=pairs[:, h], in_=moved[key, h][:].rearrange("p t u c -> p t c u"))


        def quantize(key, fmt, c0=0, c1=N):
            if c0 == 0:
                codes = stage.tile([P, N], U32, name="codes_" + key[0], align_bytes=64)
                scales = stage.tile([P, N], U8, name="scales_" + key[0], align_bytes=64)
                quant[key] = (codes, scales, fmt)
            codes, scales = quant[key][:2]
            nc.vector.quantize_mx(
                out=codes[:, c0:c1].bitcast(fmt), scales=scales[:, c0:c1], in_=staged[key][:, PACK * c0 : PACK * c1]
            )

        def mx_pass(acc, lhs_key, block, rhs_key):
            lhs_codes, lhs_scales, lhs_fmt = quant[lhs_key]
            rhs_codes, rhs_scales, rhs_fmt = quant[rhs_key]
            cols = slice(block * P, (block + 1) * P)
            nc.tensor.matmul_mx(
                out=acc[:],
                lhsT=lhs_codes[:, cols].bitcast(lhs_fmt),
                lhsT_scale=lhs_scales[:, cols],
                rhs=rhs_codes[:].bitcast(rhs_fmt),
                rhs_scale=rhs_scales[:],
                start=True,
                stop=True,
            )

        def dl_matmul(g, t, bank):
            dl_ps[g, t] = open_bank(bank, [P, N])
            mx_pass(dl_ps[g, t], ("gT", g), t, ("xT", g))

        def dx_matmul(g, s, bank):
            dx_ps[g, s] = open_bank(bank, [P, D])
            mx_pass(dx_ps[g, s], ("L", g), s, ("gI", g))


        def spread_r(g):
            r_ps[g] = open_bank(R_BANK, [P, PACK, P])
            r_col = r_first[:, 0, :] if g == 0 else r_rest[:, g - 1, :]
            for s in range(PACK):
                nc.tensor.transpose(r_ps[g][:, s, :], r_col[:, s : s + 1].to_broadcast([P, P]), ident[:])

        def copy_r_row(g):
            r_row[g] = stage.tile([P, P, PACK], F32, name="r_row")
            nc.scalar.copy(out=r_row[g][:], in_=r_ps[g][:].rearrange("p s c -> p c s"))


        def scale_adj(g, t):
            if t == 0:
                neg_m[g] = work.tile([P, 2, PACK, HALF, P], F32, name="neg_m")
            nc.vector.scalar_tensor_tensor(
                out=neg_m[g][:, :, t],
                in0=a_sb[g][:, t, :].rearrange("p (c h s) -> p h s c", h=2, s=HALF),
                scalar=neg_r[:, g, t : t + 1],
                in1=r_ps[g][:].rearrange("p (h s) c -> p h s c", h=2),
                op0=ALU.mult,
                op1=ALU.mult,
            )

        def form_laplacian(g, h):
            blocks = neg_m[g][:, h].rearrange("p t s c -> p (t s) c")
            first = HALF * HALF * h
            diagonal = blocks[:, first : first + HALF + 2 : HALF + 1, :]
            nc.gpsimd.tensor_tensor(
                out=diagonal, in0=diagonal, in1=ident[:].unsqueeze(1).to_broadcast([P, HALF, P]), op=ALU.add
            )
            if h == 0:
                staged["L", g] = stage.tile([P, PACK * N], BF16, name="st_L", align_bytes=64)
            half_out = staged["L", g][:, h * HALF * N : (h + 1) * HALF * N]
            nc.scalar.copy(
                out=half_out.rearrange("p (c i t) -> p c t i", i=RUN, t=PACK),
                in_=neg_m[g][:, h].rearrange("p t s c -> p t (s c)").rearrange("p t (c i) -> p c t i", i=RUN),
            )


        def open_interleaved(g, name):
            staged["gI", g] = stage.tile([P, PACK * D], BF16, name=name, bufs=1, align_bytes=64)

        def interleave_scalar(g, cols):
            nc.scalar.copy(
                out=staged["gI", g][:, 0 : PACK * cols].rearrange("p (c i t) -> p c t i", i=RUN, t=PACK),
                in_=g_sb[g][:, :, 0:cols].rearrange("p t (c i) -> p c t i", i=RUN),
            )

        def interleave_gpsimd(g, cols):
            nc.gpsimd.tensor_scalar(
                out=staged["gI", g][:, PACK * cols : PACK * D].rearrange("p (w t) -> p w t", t=PACK),
                in0=g_sb[g][:, :, cols:D].rearrange("p t w -> p w t"),
                scalar1=1.0,
                scalar2=0.0,
                op0=ALU.mult,
                op1=ALU.add,
            )


        def weigh_dl(g, t):
            if t == 0:
                row_sum[g] = stage.tile([P, PACK], F32, name="row_sum")
            weighed[g, t] = prod.tile([P, N], F32, name="weighed")
            nc.vector.scalar_tensor_tensor(
                out=weighed[g, t][:].rearrange("p (h w) -> p h w", h=2),
                in0=dl_ps[g, t][:].rearrange("p (h w) -> p h w", h=2),
                scalar=1.0,
                in1=neg_m[g][:, :, t].rearrange("p h s c -> p h (s c)"),
                op0=ALU.mult,
                op1=ALU.mult,
                accum_out=row_sum[g][:, t : t + 1],
            )

        def scale_dl(g, t):
            if t == 0:
                d_adj[g] = work.tile([P, PACK, N], F32, name="d_adj")
            nc.vector.tensor_tensor(
                out=d_adj[g][:, t, :].rearrange("p (c s) -> p c s", s=PACK),
                in0=dl_ps[g, t][:].rearrange("p (s c) -> p c s", s=PACK),
                in1=r_row[g][:],
                op=ALU.mult,
            )

        def column_sums(g, t):
            if t == 0:
                sum_ps[g] = open_bank(SUM_BANK, [P, PACK, SUM_WIDTH])
            for s in range(PACK):
                nc.tensor.matmul(
                    sum_ps[g][:, s, :],
                    lhsT=weighed[g, t][:, s * P : (s + 1) * P],
                    rhs=ones[:],
                    start=(t == 0 and s == 0),
                    stop=False,
                )
            if t == PACK - 1:
                nc.tensor.matmul(sum_ps[g][:, :, 0], lhsT=ident[:], rhs=row_sum[g][:], start=False, stop=True)

        def degree_term_scalar(g):
            dd[g] = stage.tile([P, PACK], F32, name="dd")
            for t in range(PACK):
                nc.scalar.activation(
                    out=dd[g][:, t : t + 1], in_=sum_ps[g][:, t, 0:1], func=ACT.Copy, scale=dd_gain[:, g, t : t + 1]
                )

        def degree_term_vector(g):
            dd[g] = stage.tile([P, PACK], F32, name="dd")
            nc.vector.tensor_tensor(out=dd[g][:], in0=sum_ps[g][:, :, 0], in1=dd_gain[:, g, :], op=ALU.mult)

        def finish_adj_scalar(g, t):
            nc.scalar.activation(
                out=d_adj[g][:, t, :],
                in_=d_adj[g][:, t, :],
                func=ACT.Identity,
                scale=neg_r[:, g, t : t + 1],
                bias=dd[g][:, t : t + 1],
            )

        def finish_adj(engine, g, t):
            engine.tensor_scalar(
                out=d_adj[g][:, t, :],
                in0=d_adj[g][:, t, :],
                scalar1=neg_r[:, g, t : t + 1],
                scalar2=dd[g][:, t : t + 1],
                op0=ALU.mult,
                op1=ALU.add,
            )

        def store_adj(g, t0, t1):
            nc.sync.dma_start(out=rows(out_1, g)[:, t0:t1, :], in_=d_adj[g][:, t0:t1, :])

        def copy_dx_out(copy, g, s):
            if s == 0:
                dx_sb[g] = work.tile([P, PACK, D], F32, name="dx_sb")
            copy(out=dx_sb[g][:, s, :], in_=dx_ps[g, s][:])

        def store_dx(g, s0, s1):
            nc.sync.dma_start(out=rows(out_0, g)[:, s0:s1, :], in_=dx_sb[g][:, s0:s1, :])

        node_constants(r_first, slice(0, 1))
        spread_r(0)
        for move in moves(0):
            transpose_pairs(move)
            copy_pairs_out(move)
        for t in range(PACK - 1):
            scale_adj(0, t)
        quantize(("xT", 0), E4M3)
        quantize(("gT", 0), E5M2, 0, HALF * P)
        for t in range(HALF):
            dl_matmul(0, t, DL_BANK + t)
        scale_adj(0, PACK - 1)
        copy_r_row(0)
        quantize(("gT", 0), E5M2, HALF * P, N)
        node_constants(r_rest, slice(1, B))
        open_interleaved(0, "st_gI")
        interleave_scalar(0, SCALAR_COLS)
        spread_r(1)
        copy_r_row(1)
        catch_up = moves(1) + moves(2)
        for t in range(PACK):
            weigh_dl(0, t)
            scale_dl(0, t)
            if t < HALF:
                dl_matmul(0, t + HALF, DL_BANK + t)
            if t > 0:
                for move in catch_up[HALF * (t - 1) : HALF * t]:
                    transpose_pairs(move)
            column_sums(0, t)
            if t == HALF - 1:
                form_laplacian(0, 0)
                interleave_gpsimd(0, SCALAR_COLS)
            if 0 < t <= HALF:
                for move in catch_up[HALF * (t - 1) : HALF * t]:
                    copy_pairs_out(move)
        load(AHEAD)

        last = B - 1
        for g in range(1, last):
            prev, nxt = g - 1, g + 1
            if g + AHEAD < B:
                load(g + AHEAD)
            form_laplacian(prev, 1)
            for t in range(PACK - 1):
                scale_adj(g, t)
            quantize(("xT", g), E4M3)
            quantize(("gT", g), E5M2)
            for t in range(HALF):
                dl_matmul(g, t, DL_BANK + t)
            if g == 1:
                for move in catch_up[PACK + HALF :]:
                    transpose_pairs(move)
            scale_adj(g, PACK - 1)
            spread_r(nxt)
            for move in moves(nxt)[:HALF]:
                copy_pairs_out(move)
            degree_term_scalar(prev)
            for move in moves(nxt)[HALF:]:
                copy_pairs_out(move)
            quantize(("L", prev), E4M3)
            quantize(("gI", prev), E5M2)
            for s in range(PACK):
                dx_matmul(prev, s, s)
            for t in range(HALF):
                finish_adj_scalar(prev, t)
            store_adj(prev, 0, HALF)
            copy_r_row(nxt)
            for h in range(2):
                for s in range(HALF * h, HALF * (h + 1)):
                    copy_dx_out(nc.scalar.copy, prev, s)
                store_dx(prev, HALF * h, HALF * (h + 1))
            open_interleaved(g, "st_gI")
            interleave_gpsimd(g, SCALAR_COLS)
            interleave_scalar(g, SCALAR_COLS)
            for t in range(HALF):
                weigh_dl(g, t)
                scale_dl(g, t)
                dl_matmul(g, t + HALF, DL_BANK + t)
                column_sums(g, t)
                if t == HALF - 1:
                    form_laplacian(g, 0)
                finish_adj(nc.gpsimd, prev, t + HALF)
            store_adj(prev, HALF, PACK)
            for h in range(2):
                weigh_dl(g, HALF + h)
                scale_dl(g, HALF + h)
                if g + 2 < B:
                    for move in moves(g + 2)[HALF * h : HALF * (h + 1)]:
                        transpose_pairs(move)
                column_sums(g, HALF + h)

        g, prev = last, last - 1

        def dx_block_out(copy, graph, s):
            copy_dx_out(copy, graph, s)
            store_dx(graph, s, s + 1)

        def adj_slot_out(engine, t):
            finish_adj(engine, g, t)
            store_adj(g, t, t + 1)

        def dx_half(h, banks):
            quantize(("L", g), E4M3, h * HALF * P, (h + 1) * HALF * P)
            for s, bank in enumerate(banks):
                dx_matmul(g, HALF * h + s, bank)

        form_laplacian(prev, 1)
        open_interleaved(g, "st_gI_last")
        interleave_gpsimd(g, SCALAR_COLS_LAST)
        degree_term_scalar(prev)
        for t in range(PACK):
            finish_adj_scalar(prev, t)
            store_adj(prev, t, t + 1)
        interleave_scalar(g, SCALAR_COLS_LAST)
        for t in range(PACK):
            scale_adj(g, t)
        quantize(("xT", g), E4M3)
        quantize(("gT", g), E5M2)
        for t, bank in enumerate((DL_BANK, DL_BANK + 1, R_BANK, PACK - 1)):
            dl_matmul(g, t, bank)
        quantize(("L", prev), E4M3)
        quantize(("gI", prev), E5M2)
        for s in range(PACK - 1):
            dx_matmul(prev, s, s)
        weigh_dl(g, 0)
        column_sums(g, 0)
        dx_block_out(nc.scalar.copy, prev, 0)
        dx_matmul(prev, PACK - 1, 0)
        for t in range(1, PACK):
            dx_block_out(nc.scalar.copy, prev, t)
            if t == HALF:
                form_laplacian(g, 0)
            if t < PACK - 1:
                weigh_dl(g, t)
                column_sums(g, t)
        weigh_dl(g, PACK - 1)
        column_sums(g, PACK - 1)
        form_laplacian(g, 1)
        for t in range(HALF):
            scale_dl(g, t)
        quantize(("gI", g), E5M2)
        dx_half(0, (1, 2))
        degree_term_vector(g)
        scale_dl(g, HALF)
        for t in range(HALF):
            adj_slot_out(nc.vector, t)
        dx_block_out(nc.scalar.copy, g, 0)
        dx_half(1, (0, DL_BANK))
        adj_slot_out(nc.vector, HALF)
        scale_dl(g, PACK - 1)
        for s in range(1, PACK - 1):
            dx_block_out(nc.scalar.copy, g, s)
        adj_slot_out(nc.gpsimd, PACK - 1)
        dx_block_out(nc.vector.tensor_copy, g, PACK - 1)
